import numpy as np
import ml_dtypes


def mxq(x, axis, fmt="e4m3"):
    dtype, down = {"e4m3": (ml_dtypes.float8_e4m3fn, 7), "e5m2": (ml_dtypes.float8_e5m2, 14)}[fmt]
    v = np.moveaxis(np.asarray(x, np.float32).astype(ml_dtypes.bfloat16).astype(np.float64), axis, -1)
    blocks = v.reshape(v.shape[:-1] + (-1, 32))
    amax = np.abs(blocks).max(-1, keepdims=True)
    byte = np.maximum(np.where(amax > 0, np.frexp(amax)[1] - 1 + 127, 0) - down, 1)
    scale = np.exp2(byte - 127.0)
    codes = (blocks / scale).astype(np.float32).astype(dtype).astype(np.float64)
    return np.moveaxis((codes * scale).reshape(v.shape), -1, axis)


WIDE = False


def mx_kscale(k):
    if not WIDE:
        return np.ones(k)
    levels = np.array([10, -10, 5, -5, 0])
    a = np.random.permutation(np.resize(levels, k // 512 * 4)).reshape(k // 512, 4)
    idx = np.arange(k)
    return np.exp2(a[idx // 512, idx % 128 // 32])


BF16 = ml_dtypes.bfloat16


def bf(x):
    return np.asarray(x, np.float32).astype(BF16)


def f64(x):
    return np.asarray(x).astype(np.float64)


B, S, E, H, C = 8, 1024, 512, 4, 512
HD = E // H
EPS = 1e-5


def silu(v):
    return v / (1.0 + np.exp(-v))


def setup_inputs():
    s, t = mx_kscale(E), mx_kscale(E)
    spread = np.exp(0.7 * np.random.standard_normal((B, S, H, 1)))
    shift = 0.5 * np.random.standard_normal((B, S, H, 1))
    attn = 1.5 * (np.random.standard_normal((B, S, H, HD)) * spread + shift)
    return {"x": bf(np.random.standard_normal((B, S, E)) * s),
            "attn": bf(attn.reshape(B, S, E)),
            "Wg": bf(np.random.standard_normal((E, E)) / np.sqrt(E) / s[:, None]),
            "bg": bf(np.random.standard_normal(E) * 0.2),
            "gn_w": bf((1.0 + 0.1 * np.random.standard_normal(E)) * t),
            "gn_b": bf(0.1 * np.random.standard_normal(E) * t),
            "Wo": bf(np.random.standard_normal((E, E)) * 1.5 / np.sqrt(E) / t[:, None]),
            "bo": bf(np.random.standard_normal(E) * 0.1)}


def reference(x, attn, Wg, bg, gn_w, gn_b, Wo, bo):
    g = f64(attn).reshape(B, S, H, HD)
    mu = g.mean(-1, keepdims=True)
    var = g.var(-1, keepdims=True)
    g = (g - mu) / np.sqrt(var + EPS)
    g = g.reshape(B, S, E) * f64(gn_w) + f64(gn_b)
    gate = silu((mxq(f64(x), 2, "e4m3") @ mxq(f64(Wg), 0, "e4m3")) + f64(bg))
    h = gate * g
    return (mxq(h, 2, "e4m3") @ mxq(f64(Wo), 0, "e4m3")) + f64(bo)

@@ -1,0 +1,220 @@
+from contextlib import ExitStack
+
+import concourse.mybir as mybir
+from concourse.masks import make_identity
+
+F32 = mybir.dt.float32
+BF16 = mybir.dt.bfloat16
+U32 = mybir.dt.uint32
+U8 = mybir.dt.uint8
+FP8X4 = mybir.dt.float8_e4m3fn_x4
+ACT = mybir.ActivationFunctionType
+ALU = mybir.AluOpType
+
+P = 128
+E = 512
+T = 8192
+G = 4
+J = 4
+MT = P * J
+NM = T // MT
+EPS = 1e-5
+FLOPS = 2 * 2 * T * E * E
+
+S_NORM_GROUPS = 3
+PIN = False
+
+
+def regroup_and_quantise(nc, pool, raw, codes, scales, name):
+    grouped = pool.tile([P, 4 * E], BF16, name=name, align_bytes=64)
+    nc.vector.tensor_copy(
+        out=grouped[:].rearrange("p (c i t) -> p c t i", i=4, t=4),
+        in_=raw[:].rearrange("p t (c i) -> p c t i", i=4),
+    )
+    nc.vector.quantize_mx(out=codes[:].bitcast(FP8X4), scales=scales[:], in_=grouped[:])
+
+
+def tile_multiscaleretention_pb_t_kernel(tc, x, attn, Wg, bg, gn_w, gn_b, Wo, bo, out):
+    nc = tc.nc
+    xf = x.flatten_outer_dims()
+    af = attn.flatten_outer_dims()
+    of = out.flatten_outer_dims()
+    with ExitStack() as ctx:
+        const = ctx.enter_context(tc.tile_pool(name="const", bufs=1))
+        xin = ctx.enter_context(tc.tile_pool(name="xin", bufs=3))
+        ain = ctx.enter_context(tc.tile_pool(name="ain", bufs=4))
+        small = ctx.enter_context(tc.tile_pool(name="small", bufs=3))
+        work = ctx.enter_context(tc.tile_pool(name="work", bufs=2))
+        outp = ctx.enter_context(tc.tile_pool(name="outp", bufs=3))
+        psum = ctx.enter_context(tc.psum_pool(name="psum", bufs=2))
+
+        x_t = {}
+        a_t = {}
+
+        def load(m):
+            x_sb = xin.tile([P, J, E], BF16)
+            nc.sync.dma_start(out=x_sb[:], in_=xf[m * MT : (m + 1) * MT, :].rearrange("(p j) k -> p j k", j=J))
+            a_sb = ain.tile([P, J, E], BF16)
+            nc.sync.dma_start(out=a_sb[:], in_=af[m * MT : (m + 1) * MT, :].rearrange("(p j) k -> p j k", j=J))
+            x_t[m] = x_sb
+            a_t[m] = a_sb
+
+        wg_raw = const.tile([P, 4, E], BF16)
+        for u in range(2):
+            nc.sync.dma_start(
+                out=wg_raw[:, 2 * u : 2 * u + 2, :],
+                in_=Wg[256 * u : 256 * u + 256, :].rearrange("(q e) c -> q e c", e=2),
+            )
+        load(0)
+        vrows = const.tile([P, P], BF16)
+        nc.vector.memset(vrows[:], 0.0)
+        nc.sync.dma_start(out=vrows[0:4, :], in_=bg.rearrange("(t p) -> t p", p=P))
+        nc.sync.dma_start(out=vrows[4:8, :], in_=gn_w.rearrange("(t p) -> t p", p=P))
+        nc.sync.dma_start(out=vrows[8:12, :], in_=gn_b.rearrange("(t p) -> t p", p=P))
+        wo_raw = const.tile([P, 4, E], BF16)
+        nc.sync.dma_start(out=wo_raw[:], in_=Wo.rearrange("(t p) n -> p t n", p=P))
+        load(1)
+        bo_bf = const.tile([P, E], BF16)
+        nc.sync.dma_start(out=bo_bf[:], in_=bo.partition_broadcast(P))
+
+        ident = const.tile([P, P], F32)
+        make_identity(nc, ident[:])
+        mhalf = const.tile([P, G * J], F32)
+        nc.vector.memset(mhalf[:], -0.5)
+
+        wg_c = const.tile([P, E], U32, align_bytes=64)
+        wg_s = const.tile([P, E], U8, align_bytes=64)
+        regroup_and_quantise(nc, const, wg_raw, wg_c, wg_s, "wg_grouped")
+        wo_c = const.tile([P, E], U32, align_bytes=64)
+        wo_s = const.tile([P, E], U8, align_bytes=64)
+        regroup_and_quantise(nc, const, wo_raw, wo_c, wo_s, "wo_grouped")
+
+        vrows32 = const.tile([P, P], F32)
+        nc.vector.tensor_copy(out=vrows32[:], in_=vrows[:])
+        vps = psum.tile([P, E], F32, tag="xt")
+        nc.tensor.transpose(vps[:, 0:P], vrows32[:], ident[:])
+        cols = const.tile([P, 12], F32)
+        nc.vector.tensor_copy(out=cols[:], in_=vps[:, 0:12])
+        bo_b = const.tile([P, E], F32)
+        nc.vector.tensor_copy(out=bo_b[:], in_=bo_bf[:])
+
+        xg_t = {}
+        st_t = {}
+        rs_t = {}
+        nb_t = {}
+        gate_t = {}
+        gs_t = {}
+
+        def stage_b(m):
+            x_sb = x_t[m]
+            a_sb = a_t[m]
+            xg = work.tile([P, 4 * MT], BF16, align_bytes=64)
+            xg_w = xg[:].bitcast(F32).rearrange("q (w u) -> q w u", u=2)
+            for hh in range(2):
+                xt = psum.tile([P, 2, 256], F32, tag="xt")
+                for jj in range(2):
+                    words = x_sb[:, 2 * hh + jj, :].bitcast(F32)
+                    for u in range(2):
+                        nc.tensor.transpose(xt[:, u, P * jj : P * jj + P], words[:, P * u : P * u + P], ident[:])
+                nc.scalar.copy(out=xg_w[:, 256 * hh : 256 * hh + 256, :], in_=xt[:].rearrange("q u w -> q w u"))
+            xg_t[m] = xg
+            st = small.tile([P, 2 * J, 6], F32)
+            for j in range(J):
+                for gp in range(2):
+                    nc.vector.bn_stats(
+                        out=st[:, 2 * j + gp, :],
+                        in_=a_sb[:, j, 256 * gp : 256 * gp + 256].rearrange("p (g c) -> p c g", g=2),
+                    )
+            st3 = st[:].rearrange("p i (s k) -> p (i s) k", k=3)
+            ve = small.tile([P, G * J], F32)
+            nc.gpsimd.tensor_scalar(out=ve[:], in0=st3[:, :, 2], scalar1=1.0 / P, scalar2=EPS, op0=ALU.mult, op1=ALU.add)
+            rstd = small.tile([P, G * J], F32)
+            nc.gpsimd.tensor_tensor(out=rstd[:], in0=ve[:], in1=mhalf[:], op=ALU.pow)
+            st_t[m] = st3
+            rs_t[m] = rstd
+            if S_NORM_GROUPS > 0:
+                nb = small.tile([P, G * J], F32)
+                nc.vector.scalar_tensor_tensor(
+                    out=nb[:], in0=st3[:, :, 1], scalar=-1.0, in1=rstd[:], op0=ALU.mult, op1=ALU.mult
+                )
+                nb_t[m] = nb
+
+        def stage_c(m):
+            a_sb = a_t[m]
+            xg = xg_t[m]
+            st3 = st_t[m]
+            rstd = rs_t[m]
+            xc = work.tile([P, MT], U32, align_bytes=64)
+            xs = work.tile([P, MT], U8, align_bytes=64)
+            nc.vector.quantize_mx(out=xc[:].bitcast(FP8X4), scales=xs[:], in_=xg[:])
+            nrm = work.tile([P, J, E], F32)
+            for g in range(G):
+                for j in range(J):
+                    i = G * j + g
+                    cs = slice(P * g, P * g + P)
+                    if g < S_NORM_GROUPS:
+                        nc.scalar.activation(
+                            out=nrm[:, j, cs], in_=a_sb[:, j, cs], func=ACT.Identity,
+                            bias=nb_t[m][:, i : i + 1], scale=rstd[:, i : i + 1],
+                        )
+                    else:
+                        nc.vector.tensor_scalar(
+                            out=nrm[:, j, cs], in0=a_sb[:, j, cs], scalar1=st3[:, i, 1:2], scalar2=rstd[:, i : i + 1],
+                            op0=ALU.subtract, op1=ALU.mult,
+                        )
+            gate = work.tile([P, G, MT], F32)
+            for t in range(G):
+                z = psum.tile([P, MT], F32, tag="z")
+                nc.tensor.matmul_mx(
+                    out=z[:],
+                    lhsT=wg_c[:, P * t : P * t + P].bitcast(FP8X4), lhsT_scale=wg_s[:, P * t : P * t + P],
+                    rhs=xc[:].bitcast(FP8X4), rhs_scale=xs[:], start=True, stop=True,
+                )
+                nc.scalar.activation(out=gate[:, t, :], in_=z[:], func=ACT.Silu, bias=cols[:, t : t + 1], scale=1.0)
+            gs = work.tile([P, G, MT], F32)
+            for g in range(G):
+                nt = psum.tile([P, MT], F32, tag="nt")
+                for j in range(J):
+                    nc.tensor.transpose(nt[:, P * j : P * j + P], nrm[:, j, P * g : P * g + P], ident[:])
+                nc.scalar.activation(
+                    out=gs[:, g, :], in_=nt[:], func=ACT.Identity,
+                    bias=cols[:, 8 + g : 9 + g], scale=cols[:, 4 + g : 5 + g],
+                )
+            gate_t[m] = gate
+            gs_t[m] = gs
+
+        def stage_d(m):
+            gate = gate_t[m]
+            gs = gs_t[m]
+            h = work.tile([P, 4 * MT], BF16, align_bytes=64)
+            nc.vector.tensor_tensor(
+                out=h[:].rearrange("p (c i t) -> p c t i", i=4, t=4),
+                in0=gate[:].rearrange("p t (c i) -> p c t i", i=4),
+                in1=gs[:].rearrange("p t (c i) -> p c t i", i=4),
+                op=ALU.mult,
+            )
+            hc = work.tile([P, MT], U32, align_bytes=64)
+            hs = work.tile([P, MT], U8, align_bytes=64)
+            nc.vector.quantize_mx(out=hc[:].bitcast(FP8X4), scales=hs[:], in_=h[:])
+            o_sb = outp.tile([P, J, E], F32)
+            for j in range(J):
+                o = psum.tile([P, E], F32, tag="o")
+                nc.tensor.matmul_mx(
+                    out=o[:],
+                    lhsT=hc[:, P * j : P * j + P].bitcast(FP8X4), lhsT_scale=hs[:, P * j : P * j + P],
+                    rhs=wo_c[:].bitcast(FP8X4), rhs_scale=wo_s[:], start=True, stop=True,
+                )
+                nc.vector.tensor_tensor(out=o_sb[:, j, :], in0=o[:], in1=bo_b[:], op=ALU.add)
+            nc.sync.dma_start(out=of[m * MT : (m + 1) * MT, :].rearrange("(p j) n -> p j n", j=J), in_=o_sb[:])
+
+        if PIN:
+            ctx.enter_context(tc.manual_schedule())
+        for i in range(NM + 2):
+            if i + 2 < NM:
+                load(i + 2)
+            if i < NM:
+                stage_b(i)
+            if 0 <= i - 1 < NM:
+                stage_c(i - 1)
+            if 0 <= i - 2 < NM:
+                stage_d(i - 2)

@@ -22,7 +22,7 @@ EPS = 1e-5
 FLOPS = 2 * 2 * T * E * E
 
 S_NORM_GROUPS = 3
-PIN = False
+PIN = True
 
 
 def regroup_and_quantise(nc, pool, raw, codes, scales, name):
@@ -98,123 +98,209 @@ def tile_multiscaleretention_pb_t_kernel(tc, x, attn, Wg, bg, gn_w, gn_b, Wo, bo
         bo_b = const.tile([P, E], F32)
         nc.vector.tensor_copy(out=bo_b[:], in_=bo_bf[:])
 
+        xt_t = {}
         xg_t = {}
         st_t = {}
         rs_t = {}
         nb_t = {}
+        xq_t = {}
+        nrm_t = {}
+        nt_t = {}
+        z_t = {}
         gate_t = {}
         gs_t = {}
+        h_t = {}
+        hq_t = {}
+        o_t = {}
+        ob_t = {}
 
-        def stage_b(m):
-            x_sb = x_t[m]
-            a_sb = a_t[m]
-            xg = work.tile([P, 4 * MT], BF16, align_bytes=64)
-            xg_w = xg[:].bitcast(F32).rearrange("q (w u) -> q w u", u=2)
-            for hh in range(2):
-                xt = psum.tile([P, 2, 256], F32, tag="xt")
-                for jj in range(2):
-                    words = x_sb[:, 2 * hh + jj, :].bitcast(F32)
-                    for u in range(2):
-                        nc.tensor.transpose(xt[:, u, P * jj : P * jj + P], words[:, P * u : P * u + P], ident[:])
-                nc.scalar.copy(out=xg_w[:, 256 * hh : 256 * hh + 256, :], in_=xt[:].rearrange("q u w -> q w u"))
-            xg_t[m] = xg
-            st = small.tile([P, 2 * J, 6], F32)
-            for j in range(J):
-                for gp in range(2):
-                    nc.vector.bn_stats(
-                        out=st[:, 2 * j + gp, :],
-                        in_=a_sb[:, j, 256 * gp : 256 * gp + 256].rearrange("p (g c) -> p c g", g=2),
-                    )
-            st3 = st[:].rearrange("p i (s k) -> p (i s) k", k=3)
-            ve = small.tile([P, G * J], F32)
-            nc.gpsimd.tensor_scalar(out=ve[:], in0=st3[:, :, 2], scalar1=1.0 / P, scalar2=EPS, op0=ALU.mult, op1=ALU.add)
-            rstd = small.tile([P, G * J], F32)
-            nc.gpsimd.tensor_tensor(out=rstd[:], in0=ve[:], in1=mhalf[:], op=ALU.pow)
-            st_t[m] = st3
-            rs_t[m] = rstd
-            if S_NORM_GROUPS > 0:
-                nb = small.tile([P, G * J], F32)
-                nc.vector.scalar_tensor_tensor(
-                    out=nb[:], in0=st3[:, :, 1], scalar=-1.0, in1=rstd[:], op0=ALU.mult, op1=ALU.mult
-                )
+        def ok(m):
+            return 0 <= m < NM
+
+        def x_transposes(m, hh):
+            xt = psum.tile([P, 2, 256], F32, tag="xt")
+            for jj in range(2):
+                words = x_t[m][:, 2 * hh + jj, :].bitcast(F32)
+                for u in range(2):
+                    nc.tensor.transpose(xt[:, u, P * jj : P * jj + P], words[:, P * u : P * u + P], ident[:])
+            xt_t[(m, hh)] = xt
+
+        def x_copy_out(m, hh):
+            if hh == 0:
+                xg = work.tile([P, 4 * MT], BF16, align_bytes=64)
+                xg_t[m] = xg
+            xg_w = xg_t[m][:].bitcast(F32).rearrange("q (w u) -> q w u", u=2)
+            nc.scalar.copy(out=xg_w[:, 256 * hh : 256 * hh + 256, :], in_=xt_t[(m, hh)][:].rearrange("q u w -> q w u"))
+
+        def stats(m, gp):
+            if gp == 0:
+                st = small.tile([P, 2, J, 6], F32)
+                rstd = small.tile([P, 2, 2 * J], F32)
+                nb = small.tile([P, 2, 2 * J], F32)
+                st_t[m] = st
+                rs_t[m] = rstd
                 nb_t[m] = nb
+            st = st_t[m]
+            for j in range(J):
+                nc.vector.bn_stats(
+                    out=st[:, gp, j, :],
+                    in_=a_t[m][:, j, 256 * gp : 256 * gp + 256].rearrange("p (g c) -> p c g", g=2),
+                )
+            st3 = st[:, gp, :, :].rearrange("p j (s k) -> p (j s) k", k=3)
+            ve = small.tile([P, 2 * J], F32)
+            nc.gpsimd.tensor_scalar(out=ve[:], in0=st3[:, :, 2], scalar1=1.0 / P, scalar2=EPS, op0=ALU.mult, op1=ALU.add)
+            nm = small.tile([P, 2 * J], F32)
+            nc.gpsimd.tensor_scalar(out=nm[:], in0=st3[:, :, 1], scalar1=-1.0, scalar2=0.0, op0=ALU.mult, op1=ALU.add)
+            nc.gpsimd.tensor_tensor(out=rs_t[m][:, gp, :], in0=ve[:], in1=mhalf[:, 0 : 2 * J], op=ALU.pow)
+            nc.gpsimd.tensor_tensor(out=nb_t[m][:, gp, :], in0=nm[:], in1=rs_t[m][:, gp, :], op=ALU.mult)
 
-        def stage_c(m):
-            a_sb = a_t[m]
-            xg = xg_t[m]
-            st3 = st_t[m]
-            rstd = rs_t[m]
+        def normalise(m, g):
+            if g == 0:
+                nrm = work.tile([P, J, E], F32)
+                nrm_t[m] = nrm
+            gp = g // 2
+            s = g % 2
+            cs = slice(P * g, P * g + P)
+            for j in range(J):
+                i = 2 * j + s
+                if g < S_NORM_GROUPS:
+                    nc.scalar.activation(
+                        out=nrm_t[m][:, j, cs], in_=a_t[m][:, j, cs], func=ACT.Identity,
+                        bias=nb_t[m][:, gp, i : i + 1], scale=rs_t[m][:, gp, i : i + 1],
+                    )
+                else:
+                    nc.vector.tensor_scalar(
+                        out=nrm_t[m][:, j, cs], in0=a_t[m][:, j, cs],
+                        scalar1=st_t[m][:, gp, j, 3 * s + 1 : 3 * s + 2], scalar2=rs_t[m][:, gp, i : i + 1],
+                        op0=ALU.subtract, op1=ALU.mult,
+                    )
+
+        def n_transposes(m, g):
+            nt = psum.tile([P, MT], F32, tag="nt")
+            for j in range(J):
+                nc.tensor.transpose(nt[:, P * j : P * j + P], nrm_t[m][:, j, P * g : P * g + P], ident[:])
+            nt_t[(m, g)] = nt
+
+        def gain_bias(m, g):
+            if g == 0:
+                gs = work.tile([P, G, MT], F32)
+                gs_t[m] = gs
+            nc.scalar.activation(
+                out=gs_t[m][:, g, :], in_=nt_t[(m, g)][:], func=ACT.Identity,
+                bias=cols[:, 8 + g : 9 + g], scale=cols[:, 4 + g : 5 + g],
+            )
+
+        def quantise_x(m):
             xc = work.tile([P, MT], U32, align_bytes=64)
             xs = work.tile([P, MT], U8, align_bytes=64)
-            nc.vector.quantize_mx(out=xc[:].bitcast(FP8X4), scales=xs[:], in_=xg[:])
-            nrm = work.tile([P, J, E], F32)
-            for g in range(G):
-                for j in range(J):
-                    i = G * j + g
-                    cs = slice(P * g, P * g + P)
-                    if g < S_NORM_GROUPS:
-                        nc.scalar.activation(
-                            out=nrm[:, j, cs], in_=a_sb[:, j, cs], func=ACT.Identity,
-                            bias=nb_t[m][:, i : i + 1], scale=rstd[:, i : i + 1],
-                        )
-                    else:
-                        nc.vector.tensor_scalar(
-                            out=nrm[:, j, cs], in0=a_sb[:, j, cs], scalar1=st3[:, i, 1:2], scalar2=rstd[:, i : i + 1],
-                            op0=ALU.subtract, op1=ALU.mult,
-                        )
-            gate = work.tile([P, G, MT], F32)
-            for t in range(G):
-                z = psum.tile([P, MT], F32, tag="z")
-                nc.tensor.matmul_mx(
-                    out=z[:],
-                    lhsT=wg_c[:, P * t : P * t + P].bitcast(FP8X4), lhsT_scale=wg_s[:, P * t : P * t + P],
-                    rhs=xc[:].bitcast(FP8X4), rhs_scale=xs[:], start=True, stop=True,
-                )
-                nc.scalar.activation(out=gate[:, t, :], in_=z[:], func=ACT.Silu, bias=cols[:, t : t + 1], scale=1.0)
-            gs = work.tile([P, G, MT], F32)
-            for g in range(G):
-                nt = psum.tile([P, MT], F32, tag="nt")
-                for j in range(J):
-                    nc.tensor.transpose(nt[:, P * j : P * j + P], nrm[:, j, P * g : P * g + P], ident[:])
-                nc.scalar.activation(
-                    out=gs[:, g, :], in_=nt[:], func=ACT.Identity,
-                    bias=cols[:, 8 + g : 9 + g], scale=cols[:, 4 + g : 5 + g],
-                )
-            gate_t[m] = gate
-            gs_t[m] = gs
+            nc.vector.quantize_mx(out=xc[:].bitcast(FP8X4), scales=xs[:], in_=xg_t[m][:])
+            xq_t[m] = (xc, xs)
 
-        def stage_d(m):
-            gate = gate_t[m]
-            gs = gs_t[m]
+        def matmul_1(m, t):
+            xc, xs = xq_t[m]
+            z = psum.tile([P, MT], F32, tag="z")
+            nc.tensor.matmul_mx(
+                out=z[:],
+                lhsT=wg_c[:, P * t : P * t + P].bitcast(FP8X4), lhsT_scale=wg_s[:, P * t : P * t + P],
+                rhs=xc[:].bitcast(FP8X4), rhs_scale=xs[:], start=True, stop=True,
+            )
+            z_t[(m, t)] = z
+
+        def silu(m, t):
+            if t == 0:
+                gate = work.tile([P, G, MT], F32)
+                gate_t[m] = gate
+            nc.scalar.activation(out=gate_t[m][:, t, :], in_=z_t[(m, t)][:], func=ACT.Silu, bias=cols[:, t : t + 1], scale=1.0)
+
+        def product(m):
             h = work.tile([P, 4 * MT], BF16, align_bytes=64)
             nc.vector.tensor_tensor(
                 out=h[:].rearrange("p (c i t) -> p c t i", i=4, t=4),
-                in0=gate[:].rearrange("p t (c i) -> p c t i", i=4),
-                in1=gs[:].rearrange("p t (c i) -> p c t i", i=4),
+                in0=gate_t[m][:].rearrange("p t (c i) -> p c t i", i=4),
+                in1=gs_t[m][:].rearrange("p t (c i) -> p c t i", i=4),
                 op=ALU.mult,
             )
+            h_t[m] = h
+
+        def quantise_h(m):
             hc = work.tile([P, MT], U32, align_bytes=64)
             hs = work.tile([P, MT], U8, align_bytes=64)
-            nc.vector.quantize_mx(out=hc[:].bitcast(FP8X4), scales=hs[:], in_=h[:])
-            o_sb = outp.tile([P, J, E], F32)
-            for j in range(J):
-                o = psum.tile([P, E], F32, tag="o")
-                nc.tensor.matmul_mx(
-                    out=o[:],
-                    lhsT=hc[:, P * j : P * j + P].bitcast(FP8X4), lhsT_scale=hs[:, P * j : P * j + P],
-                    rhs=wo_c[:].bitcast(FP8X4), rhs_scale=wo_s[:], start=True, stop=True,
-                )
-                nc.vector.tensor_tensor(out=o_sb[:, j, :], in0=o[:], in1=bo_b[:], op=ALU.add)
-            nc.sync.dma_start(out=of[m * MT : (m + 1) * MT, :].rearrange("(p j) n -> p j n", j=J), in_=o_sb[:])
+            nc.vector.quantize_mx(out=hc[:].bitcast(FP8X4), scales=hs[:], in_=h_t[m][:])
+            hq_t[m] = (hc, hs)
+
+        def matmul_2(m, j):
+            hc, hs = hq_t[m]
+            o = psum.tile([P, E], F32, tag="o")
+            nc.tensor.matmul_mx(
+                out=o[:],
+                lhsT=hc[:, P * j : P * j + P].bitcast(FP8X4), lhsT_scale=hs[:, P * j : P * j + P],
+                rhs=wo_c[:].bitcast(FP8X4), rhs_scale=wo_s[:], start=True, stop=True,
+            )
+            o_t[(m, j)] = o
+
+        def add_bo(m, j):
+            if j == 0:
+                o_sb = outp.tile([P, J, E], F32)
+                ob_t[m] = o_sb
+            nc.vector.tensor_tensor(out=ob_t[m][:, j, :], in0=o_t[(m, j)][:], in1=bo_b[:], op=ALU.add)
+
+        def store(m):
+            nc.sync.dma_start(out=of[m * MT : (m + 1) * MT, :].rearrange("(p j) n -> p j n", j=J), in_=ob_t[m][:])
 
         if PIN:
             ctx.enter_context(tc.manual_schedule())
+        x_transposes(0, 0)
+        x_transposes(0, 1)
         for i in range(NM + 2):
-            if i + 2 < NM:
+            b = i
+            c = i - 1
+            d = i - 2
+            if ok(i + 2):
                 load(i + 2)
-            if i < NM:
-                stage_b(i)
-            if 0 <= i - 1 < NM:
-                stage_c(i - 1)
-            if 0 <= i - 2 < NM:
-                stage_d(i - 2)
+            if ok(b):
+                stats(b, 0)
+                x_copy_out(b, 0)
+                x_copy_out(b, 1)
+            if ok(b + 1):
+                x_transposes(b + 1, 0)
+                x_transposes(b + 1, 1)
+            if ok(c):
+                normalise(c, 0)
+                n_transposes(c, 0)
+                normalise(c, 1)
+                n_transposes(c, 1)
+                normalise(c, 2)
+            if ok(d):
+                product(d)
+            if ok(c):
+                quantise_x(c)
+                normalise(c, 3)
+                gain_bias(c, 0)
+                n_transposes(c, 2)
+                matmul_1(c, 0)
+                matmul_1(c, 1)
+                gain_bias(c, 1)
+                n_transposes(c, 3)
+                gain_bias(c, 2)
+            if ok(d):
+                quantise_h(d)
+                matmul_2(d, 0)
+                matmul_2(d, 1)
+            if ok(c):
+                silu(c, 0)
+                matmul_1(c, 2)
+                silu(c, 1)
+                matmul_1(c, 3)
+                silu(c, 2)
+                silu(c, 3)
+                gain_bias(c, 3)
+            if ok(b):
+                stats(b, 1)
+            if ok(d):
+                add_bo(d, 0)
+                matmul_2(d, 2)
+                add_bo(d, 1)
+                matmul_2(d, 3)
+                add_bo(d, 2)
+                add_bo(d, 3)
+                store(d)

@@ -42,8 +42,8 @@ def tile_multiscaleretention_pb_t_kernel(tc, x, attn, Wg, bg, gn_w, gn_b, Wo, bo
     with ExitStack() as ctx:
         const = ctx.enter_context(tc.tile_pool(name="const", bufs=1))
         xin = ctx.enter_context(tc.tile_pool(name="xin", bufs=3))
-        ain = ctx.enter_context(tc.tile_pool(name="ain", bufs=4))
-        small = ctx.enter_context(tc.tile_pool(name="small", bufs=3))
+        ain = ctx.enter_context(tc.tile_pool(name="ain", bufs=6))
+        small = ctx.enter_context(tc.tile_pool(name="small", bufs=4))
         work = ctx.enter_context(tc.tile_pool(name="work", bufs=2))
         outp = ctx.enter_context(tc.tile_pool(name="outp", bufs=3))
         psum = ctx.enter_context(tc.psum_pool(name="psum", bufs=2))
@@ -51,12 +51,14 @@ def tile_multiscaleretention_pb_t_kernel(tc, x, attn, Wg, bg, gn_w, gn_b, Wo, bo
         x_t = {}
         a_t = {}
 
-        def load(m):
+        def load_x(m):
             x_sb = xin.tile([P, J, E], BF16)
             nc.sync.dma_start(out=x_sb[:], in_=xf[m * MT : (m + 1) * MT, :].rearrange("(p j) k -> p j k", j=J))
+            x_t[m] = x_sb
+
+        def load_a(m):
             a_sb = ain.tile([P, J, E], BF16)
             nc.sync.dma_start(out=a_sb[:], in_=af[m * MT : (m + 1) * MT, :].rearrange("(p j) k -> p j k", j=J))
-            x_t[m] = x_sb
             a_t[m] = a_sb
 
         wg_raw = const.tile([P, 4, E], BF16)
@@ -65,7 +67,8 @@ def tile_multiscaleretention_pb_t_kernel(tc, x, attn, Wg, bg, gn_w, gn_b, Wo, bo
                 out=wg_raw[:, 2 * u : 2 * u + 2, :],
                 in_=Wg[256 * u : 256 * u + 256, :].rearrange("(q e) c -> q e c", e=2),
             )
-        load(0)
+        load_x(0)
+        load_a(0)
         vrows = const.tile([P, P], BF16)
         nc.vector.memset(vrows[:], 0.0)
         nc.sync.dma_start(out=vrows[0:4, :], in_=bg.rearrange("(t p) -> t p", p=P))
@@ -73,7 +76,9 @@ def tile_multiscaleretention_pb_t_kernel(tc, x, attn, Wg, bg, gn_w, gn_b, Wo, bo
         nc.sync.dma_start(out=vrows[8:12, :], in_=gn_b.rearrange("(t p) -> t p", p=P))
         wo_raw = const.tile([P, 4, E], BF16)
         nc.sync.dma_start(out=wo_raw[:], in_=Wo.rearrange("(t p) n -> p t n", p=P))
-        load(1)
+        load_a(1)
+        load_x(1)
+        load_a(2)
         bo_bf = const.tile([P, E], BF16)
         nc.sync.dma_start(out=bo_bf[:], in_=bo.partition_broadcast(P))
 
@@ -132,46 +137,43 @@ def tile_multiscaleretention_pb_t_kernel(tc, x, attn, Wg, bg, gn_w, gn_b, Wo, bo
             xg_w = xg_t[m][:].bitcast(F32).rearrange("q (w u) -> q w u", u=2)
             nc.scalar.copy(out=xg_w[:, 256 * hh : 256 * hh + 256, :], in_=xt_t[(m, hh)][:].rearrange("q u w -> q w u"))
 
-        def stats(m, gp):
-            if gp == 0:
-                st = small.tile([P, 2, J, 6], F32)
-                rstd = small.tile([P, 2, 2 * J], F32)
-                nb = small.tile([P, 2, 2 * J], F32)
-                st_t[m] = st
-                rs_t[m] = rstd
-                nb_t[m] = nb
-            st = st_t[m]
+        def stats(m):
+            st = small.tile([P, J, 2, 6], F32)
             for j in range(J):
-                nc.vector.bn_stats(
-                    out=st[:, gp, j, :],
-                    in_=a_t[m][:, j, 256 * gp : 256 * gp + 256].rearrange("p (g c) -> p c g", g=2),
-                )
-            st3 = st[:, gp, :, :].rearrange("p j (s k) -> p (j s) k", k=3)
-            ve = small.tile([P, 2 * J], F32)
+                for gp in range(2):
+                    nc.vector.bn_stats(
+                        out=st[:, j, gp, :],
+                        in_=a_t[m][:, j, 256 * gp : 256 * gp + 256].rearrange("p (g c) -> p c g", g=2),
+                    )
+            st3 = st[:].rearrange("p j gp (s k) -> p (j gp s) k", k=3)
+            ve = small.tile([P, G * J], F32)
             nc.gpsimd.tensor_scalar(out=ve[:], in0=st3[:, :, 2], scalar1=1.0 / P, scalar2=EPS, op0=ALU.mult, op1=ALU.add)
-            nm = small.tile([P, 2 * J], F32)
+            nm = small.tile([P, G * J], F32)
             nc.gpsimd.tensor_scalar(out=nm[:], in0=st3[:, :, 1], scalar1=-1.0, scalar2=0.0, op0=ALU.mult, op1=ALU.add)
-            nc.gpsimd.tensor_tensor(out=rs_t[m][:, gp, :], in0=ve[:], in1=mhalf[:, 0 : 2 * J], op=ALU.pow)
-            nc.gpsimd.tensor_tensor(out=nb_t[m][:, gp, :], in0=nm[:], in1=rs_t[m][:, gp, :], op=ALU.mult)
+            rstd = small.tile([P, G * J], F32)
+            nc.gpsimd.tensor_tensor(out=rstd[:], in0=ve[:], in1=mhalf[:], op=ALU.pow)
+            nb = small.tile([P, G * J], F32)
+            nc.gpsimd.tensor_tensor(out=nb[:], in0=nm[:], in1=rstd[:], op=ALU.mult)
+            st_t[m] = st3
+            rs_t[m] = rstd
+            nb_t[m] = nb
 
         def normalise(m, g):
             if g == 0:
                 nrm = work.tile([P, J, E], F32)
                 nrm_t[m] = nrm
-            gp = g // 2
-            s = g % 2
             cs = slice(P * g, P * g + P)
             for j in range(J):
-                i = 2 * j + s
+                i = G * j + g
                 if g < S_NORM_GROUPS:
                     nc.scalar.activation(
                         out=nrm_t[m][:, j, cs], in_=a_t[m][:, j, cs], func=ACT.Identity,
-                        bias=nb_t[m][:, gp, i : i + 1], scale=rs_t[m][:, gp, i : i + 1],
+                        bias=nb_t[m][:, i : i + 1], scale=rs_t[m][:, i : i + 1],
                     )
                 else:
                     nc.vector.tensor_scalar(
                         out=nrm_t[m][:, j, cs], in0=a_t[m][:, j, cs],
-                        scalar1=st_t[m][:, gp, j, 3 * s + 1 : 3 * s + 2], scalar2=rs_t[m][:, gp, i : i + 1],
+                        scalar1=st_t[m][:, i, 1:2], scalar2=rs_t[m][:, i : i + 1],
                         op0=ALU.subtract, op1=ALU.mult,
                     )
 
@@ -249,21 +251,19 @@ def tile_multiscaleretention_pb_t_kernel(tc, x, attn, Wg, bg, gn_w, gn_b, Wo, bo
 
         if PIN:
             ctx.enter_context(tc.manual_schedule())
-        x_transposes(0, 0)
-        x_transposes(0, 1)
-        for i in range(NM + 2):
-            b = i
+        for i in range(-1, NM + 2):
             c = i - 1
             d = i - 2
-            if ok(i + 2):
-                load(i + 2)
-            if ok(b):
-                stats(b, 0)
-                x_copy_out(b, 0)
-                x_copy_out(b, 1)
-            if ok(b + 1):
-                x_transposes(b + 1, 0)
-                x_transposes(b + 1, 1)
+            if ok(i + 2) and i + 2 >= 2:
+                load_x(i + 2)
+            if ok(i + 3) and i + 3 >= 3:
+                load_a(i + 3)
+            if ok(i):
+                x_copy_out(i, 0)
+                x_copy_out(i, 1)
+            if ok(i + 1):
+                x_transposes(i + 1, 0)
+                x_transposes(i + 1, 1)
             if ok(c):
                 normalise(c, 0)
                 n_transposes(c, 0)
@@ -275,18 +275,18 @@ def tile_multiscaleretention_pb_t_kernel(tc, x, attn, Wg, bg, gn_w, gn_b, Wo, bo
             if ok(c):
                 quantise_x(c)
                 normalise(c, 3)
-                gain_bias(c, 0)
-                n_transposes(c, 2)
                 matmul_1(c, 0)
                 matmul_1(c, 1)
-                gain_bias(c, 1)
-                n_transposes(c, 3)
-                gain_bias(c, 2)
+                gain_bias(c, 0)
+                n_transposes(c, 2)
             if ok(d):
                 quantise_h(d)
                 matmul_2(d, 0)
                 matmul_2(d, 1)
             if ok(c):
+                gain_bias(c, 1)
+                n_transposes(c, 3)
+                gain_bias(c, 2)
                 silu(c, 0)
                 matmul_1(c, 2)
                 silu(c, 1)
@@ -294,8 +294,8 @@ def tile_multiscaleretention_pb_t_kernel(tc, x, attn, Wg, bg, gn_w, gn_b, Wo, bo
                 silu(c, 2)
                 silu(c, 3)
                 gain_bias(c, 3)
-            if ok(b):
-                stats(b, 1)
+            if ok(i + 1):
+                stats(i + 1)
             if ok(d):
                 add_bo(d, 0)
                 matmul_2(d, 2)

@@ -23,6 +23,7 @@ FLOPS = 2 * 2 * T * E * E
 
 S_NORM_GROUPS = 3
 PIN = True
+LA = 2
 
 
 def regroup_and_quantise(nc, pool, raw, codes, scales, name):
@@ -42,11 +43,11 @@ def tile_multiscaleretention_pb_t_kernel(tc, x, attn, Wg, bg, gn_w, gn_b, Wo, bo
     with ExitStack() as ctx:
         const = ctx.enter_context(tc.tile_pool(name="const", bufs=1))
         xin = ctx.enter_context(tc.tile_pool(name="xin", bufs=3))
-        ain = ctx.enter_context(tc.tile_pool(name="ain", bufs=6))
-        small = ctx.enter_context(tc.tile_pool(name="small", bufs=4))
+        ain = ctx.enter_context(tc.tile_pool(name="ain", bufs=LA + 5))
+        small = ctx.enter_context(tc.tile_pool(name="small", bufs=LA + 3))
         work = ctx.enter_context(tc.tile_pool(name="work", bufs=2))
         outp = ctx.enter_context(tc.tile_pool(name="outp", bufs=3))
-        psum = ctx.enter_context(tc.psum_pool(name="psum", bufs=2))
+        psum = ctx.enter_context(tc.psum_pool(name="psum", bufs=4))
 
         x_t = {}
         a_t = {}
@@ -78,7 +79,8 @@ def tile_multiscaleretention_pb_t_kernel(tc, x, attn, Wg, bg, gn_w, gn_b, Wo, bo
         nc.sync.dma_start(out=wo_raw[:], in_=Wo.rearrange("(t p) n -> p t n", p=P))
         load_a(1)
         load_x(1)
-        load_a(2)
+        for m in range(2, LA + 2):
+            load_a(m)
         bo_bf = const.tile([P, E], BF16)
         nc.sync.dma_start(out=bo_bf[:], in_=bo.partition_broadcast(P))
 
@@ -96,7 +98,7 @@ def tile_multiscaleretention_pb_t_kernel(tc, x, attn, Wg, bg, gn_w, gn_b, Wo, bo
 
         vrows32 = const.tile([P, P], F32)
         nc.vector.tensor_copy(out=vrows32[:], in_=vrows[:])
-        vps = psum.tile([P, E], F32, tag="xt")
+        vps = psum.tile([P, E], F32, tag="s")
         nc.tensor.transpose(vps[:, 0:P], vrows32[:], ident[:])
         cols = const.tile([P, 12], F32)
         nc.vector.tensor_copy(out=cols[:], in_=vps[:, 0:12])
@@ -123,7 +125,7 @@ def tile_multiscaleretention_pb_t_kernel(tc, x, attn, Wg, bg, gn_w, gn_b, Wo, bo
             return 0 <= m < NM
 
         def x_transposes(m, hh):
-            xt = psum.tile([P, 2, 256], F32, tag="xt")
+            xt = psum.tile([P, 2, 256], F32, tag="s")
             for jj in range(2):
                 words = x_t[m][:, 2 * hh + jj, :].bitcast(F32)
                 for u in range(2):
@@ -178,7 +180,7 @@ def tile_multiscaleretention_pb_t_kernel(tc, x, attn, Wg, bg, gn_w, gn_b, Wo, bo
                     )
 
         def n_transposes(m, g):
-            nt = psum.tile([P, MT], F32, tag="nt")
+            nt = psum.tile([P, MT], F32, tag="s")
             for j in range(J):
                 nc.tensor.transpose(nt[:, P * j : P * j + P], nrm_t[m][:, j, P * g : P * g + P], ident[:])
             nt_t[(m, g)] = nt
@@ -200,7 +202,7 @@ def tile_multiscaleretention_pb_t_kernel(tc, x, attn, Wg, bg, gn_w, gn_b, Wo, bo
 
         def matmul_1(m, t):
             xc, xs = xq_t[m]
-            z = psum.tile([P, MT], F32, tag="z")
+            z = psum.tile([P, MT], F32, tag="s")
             nc.tensor.matmul_mx(
                 out=z[:],
                 lhsT=wg_c[:, P * t : P * t + P].bitcast(FP8X4), lhsT_scale=wg_s[:, P * t : P * t + P],
@@ -251,56 +253,59 @@ def tile_multiscaleretention_pb_t_kernel(tc, x, attn, Wg, bg, gn_w, gn_b, Wo, bo
 
         if PIN:
             ctx.enter_context(tc.manual_schedule())
-        for i in range(-1, NM + 2):
+        for i in range(-LA, NM + 2):
             c = i - 1
             d = i - 2
-            if ok(i + 2) and i + 2 >= 2:
+            if ok(i + 2) and i >= 0:
                 load_x(i + 2)
-            if ok(i + 3) and i + 3 >= 3:
-                load_a(i + 3)
+            if ok(i + LA + 2) and i >= 0:
+                load_a(i + LA + 2)
             if ok(i):
                 x_copy_out(i, 0)
                 x_copy_out(i, 1)
-            if ok(i + 1):
-                x_transposes(i + 1, 0)
-                x_transposes(i + 1, 1)
             if ok(c):
                 normalise(c, 0)
                 n_transposes(c, 0)
                 normalise(c, 1)
                 n_transposes(c, 1)
                 normalise(c, 2)
+                n_transposes(c, 2)
             if ok(d):
                 product(d)
             if ok(c):
                 quantise_x(c)
                 normalise(c, 3)
-                matmul_1(c, 0)
-                matmul_1(c, 1)
+                n_transposes(c, 3)
                 gain_bias(c, 0)
-                n_transposes(c, 2)
+                matmul_1(c, 0)
+                gain_bias(c, 1)
+                matmul_1(c, 1)
+                gain_bias(c, 2)
+                matmul_1(c, 2)
             if ok(d):
                 quantise_h(d)
                 matmul_2(d, 0)
                 matmul_2(d, 1)
             if ok(c):
-                gain_bias(c, 1)
-                n_transposes(c, 3)
-                gain_bias(c, 2)
-                silu(c, 0)
-                matmul_1(c, 2)
-                silu(c, 1)
+                gain_bias(c, 3)
                 matmul_1(c, 3)
+            if ok(d):
+                matmul_2(d, 2)
+                matmul_2(d, 3)
+            if ok(c):
+                silu(c, 0)
+            if ok(i + 1) and i >= -1:
+                x_transposes(i + 1, 0)
+            if ok(c):
+                silu(c, 1)
+            if ok(i + 1) and i >= -1:
+                x_transposes(i + 1, 1)
+            if ok(c):
                 silu(c, 2)
                 silu(c, 3)
-                gain_bias(c, 3)
-            if ok(i + 1):
-                stats(i + 1)
+            if ok(i + LA):
+                stats(i + LA)
             if ok(d):
-                add_bo(d, 0)
-                matmul_2(d, 2)
-                add_bo(d, 1)
-                matmul_2(d, 3)
-                add_bo(d, 2)
-                add_bo(d, 3)
+                for j in range(J):
+                    add_bo(d, j)
                 store(d)

@@ -21,7 +21,8 @@ NM = T // MT
 EPS = 1e-5
 FLOPS = 2 * 2 * T * E * E
 
-S_NORM_GROUPS = 3
+S_NORM = 10
+TV = 256
 PIN = True
 LA = 2
 
@@ -47,6 +48,7 @@ def tile_multiscaleretention_pb_t_kernel(tc, x, attn, Wg, bg, gn_w, gn_b, Wo, bo
         small = ctx.enter_context(tc.tile_pool(name="small", bufs=LA + 3))
         work = ctx.enter_context(tc.tile_pool(name="work", bufs=2))
         outp = ctx.enter_context(tc.tile_pool(name="outp", bufs=3))
+        single = ctx.enter_context(tc.tile_pool(name="single", bufs=1))
         psum = ctx.enter_context(tc.psum_pool(name="psum", bufs=4))
 
         x_t = {}
@@ -88,6 +90,8 @@ def tile_multiscaleretention_pb_t_kernel(tc, x, attn, Wg, bg, gn_w, gn_b, Wo, bo
         make_identity(nc, ident[:])
         mhalf = const.tile([P, G * J], F32)
         nc.vector.memset(mhalf[:], -0.5)
+        eps_col = const.tile([P, 1], F32)
+        nc.vector.memset(eps_col[:], EPS)
 
         wg_c = const.tile([P, E], U32, align_bytes=64)
         wg_s = const.tile([P, E], U8, align_bytes=64)
@@ -147,16 +151,18 @@ def tile_multiscaleretention_pb_t_kernel(tc, x, attn, Wg, bg, gn_w, gn_b, Wo, bo
                         out=st[:, j, gp, :],
                         in_=a_t[m][:, j, 256 * gp : 256 * gp + 256].rearrange("p (g c) -> p c g", g=2),
                     )
-            st3 = st[:].rearrange("p j gp (s k) -> p (j gp s) k", k=3)
+            st_t[m] = st[:].rearrange("p j gp (s k) -> p (j gp s) k", k=3)
+
+        def rstd_ops(m):
+            st3 = st_t[m]
             ve = small.tile([P, G * J], F32)
-            nc.gpsimd.tensor_scalar(out=ve[:], in0=st3[:, :, 2], scalar1=1.0 / P, scalar2=EPS, op0=ALU.mult, op1=ALU.add)
+            nc.scalar.activation(out=ve[:], in_=st3[:, :, 2], func=ACT.Identity, bias=eps_col[:], scale=1.0 / P)
             nm = small.tile([P, G * J], F32)
-            nc.gpsimd.tensor_scalar(out=nm[:], in0=st3[:, :, 1], scalar1=-1.0, scalar2=0.0, op0=ALU.mult, op1=ALU.add)
+            nc.scalar.mul(out=nm[:], in_=st3[:, :, 1], mul=-1.0)
             rstd = small.tile([P, G * J], F32)
             nc.gpsimd.tensor_tensor(out=rstd[:], in0=ve[:], in1=mhalf[:], op=ALU.pow)
             nb = small.tile([P, G * J], F32)
             nc.gpsimd.tensor_tensor(out=nb[:], in0=nm[:], in1=rstd[:], op=ALU.mult)
-            st_t[m] = st3
             rs_t[m] = rstd
             nb_t[m] = nb
 
@@ -167,7 +173,7 @@ def tile_multiscaleretention_pb_t_kernel(tc, x, attn, Wg, bg, gn_w, gn_b, Wo, bo
             cs = slice(P * g, P * g + P)
             for j in range(J):
                 i = G * j + g
-                if g < S_NORM_GROUPS:
+                if G * g + j < S_NORM:
                     nc.scalar.activation(
                         out=nrm_t[m][:, j, cs], in_=a_t[m][:, j, cs], func=ACT.Identity,
                         bias=nb_t[m][:, i : i + 1], scale=rs_t[m][:, i : i + 1],
@@ -216,20 +222,31 @@ def tile_multiscaleretention_pb_t_kernel(tc, x, attn, Wg, bg, gn_w, gn_b, Wo, bo
                 gate_t[m] = gate
             nc.scalar.activation(out=gate_t[m][:, t, :], in_=z_t[(m, t)][:], func=ACT.Silu, bias=cols[:, t : t + 1], scale=1.0)
 
-        def product(m):
-            h = work.tile([P, 4 * MT], BF16, align_bytes=64)
+        def product_v(m):
+            hv = work.tile([P, 4 * TV], BF16, align_bytes=64)
             nc.vector.tensor_tensor(
-                out=h[:].rearrange("p (c i t) -> p c t i", i=4, t=4),
-                in0=gate_t[m][:].rearrange("p t (c i) -> p c t i", i=4),
-                in1=gs_t[m][:].rearrange("p t (c i) -> p c t i", i=4),
+                out=hv[:].rearrange("p (c i t) -> p c t i", i=4, t=4),
+                in0=gate_t[m][:, :, 0:TV].rearrange("p t (c i) -> p c t i", i=4),
+                in1=gs_t[m][:, :, 0:TV].rearrange("p t (c i) -> p c t i", i=4),
                 op=ALU.mult,
             )
-            h_t[m] = h
+            h_t[(m, 0)] = hv
+
+        def product_g(m):
+            hg = single.tile([P, 4 * (MT - TV)], BF16, align_bytes=64)
+            nc.gpsimd.tensor_tensor(
+                out=hg[:].rearrange("p (w t) -> p w t", t=4),
+                in0=gate_t[m][:, :, TV:MT].rearrange("p t w -> p w t"),
+                in1=gs_t[m][:, :, TV:MT].rearrange("p t w -> p w t"),
+                op=ALU.mult,
+            )
+            h_t[(m, 1)] = hg
 
         def quantise_h(m):
             hc = work.tile([P, MT], U32, align_bytes=64)
             hs = work.tile([P, MT], U8, align_bytes=64)
-            nc.vector.quantize_mx(out=hc[:].bitcast(FP8X4), scales=hs[:], in_=h_t[m][:])
+            nc.vector.quantize_mx(out=hc[:, 0:TV].bitcast(FP8X4), scales=hs[:, 0:TV], in_=h_t[(m, 0)][:])
+            nc.vector.quantize_mx(out=hc[:, TV:MT].bitcast(FP8X4), scales=hs[:, TV:MT], in_=h_t[(m, 1)][:])
             hq_t[m] = (hc, hs)
 
         def matmul_2(m, j):
@@ -253,45 +270,44 @@ def tile_multiscaleretention_pb_t_kernel(tc, x, attn, Wg, bg, gn_w, gn_b, Wo, bo
 
         if PIN:
             ctx.enter_context(tc.manual_schedule())
-        for i in range(-LA, NM + 2):
+        for i in range(-LA, NM + 3):
             c = i - 1
-            d = i - 2
+            d1 = i - 2
+            d2 = i - 3
             if ok(i + 2) and i >= 0:
                 load_x(i + 2)
             if ok(i + LA + 2) and i >= 0:
                 load_a(i + LA + 2)
+            if ok(i + LA - 1):
+                rstd_ops(i + LA - 1)
             if ok(i):
                 x_copy_out(i, 0)
                 x_copy_out(i, 1)
-            if ok(c):
-                normalise(c, 0)
-                n_transposes(c, 0)
-                normalise(c, 1)
-                n_transposes(c, 1)
-                normalise(c, 2)
-                n_transposes(c, 2)
-            if ok(d):
-                product(d)
+            if ok(d1):
+                product_v(d1)
             if ok(c):
                 quantise_x(c)
-                normalise(c, 3)
-                n_transposes(c, 3)
+                for g in range(G):
+                    normalise(c, g)
+                    n_transposes(c, g)
                 gain_bias(c, 0)
                 matmul_1(c, 0)
                 gain_bias(c, 1)
                 matmul_1(c, 1)
                 gain_bias(c, 2)
                 matmul_1(c, 2)
-            if ok(d):
-                quantise_h(d)
-                matmul_2(d, 0)
-                matmul_2(d, 1)
+            if ok(d2):
+                quantise_h(d2)
+                matmul_2(d2, 0)
+                matmul_2(d2, 1)
+            if ok(d1):
+                product_g(d1)
             if ok(c):
                 gain_bias(c, 3)
                 matmul_1(c, 3)
-            if ok(d):
-                matmul_2(d, 2)
-                matmul_2(d, 3)
+            if ok(d2):
+                matmul_2(d2, 2)
+                matmul_2(d2, 3)
             if ok(c):
                 silu(c, 0)
             if ok(i + 1) and i >= -1:
@@ -305,7 +321,7 @@ def tile_multiscaleretention_pb_t_kernel(tc, x, attn, Wg, bg, gn_w, gn_b, Wo, bo
                 silu(c, 3)
             if ok(i + LA):
                 stats(i + LA)
-            if ok(d):
+            if ok(d2):
                 for j in range(J):
-                    add_bo(d, j)
-                store(d)
+                    add_bo(d2, j)
+                store(d2)

@@ -21,19 +21,8 @@ NM = T // MT
 EPS = 1e-5
 FLOPS = 2 * 2 * T * E * E
 
-S_NORM = 10
-TV = 256
-PIN = True
-LA = 2
-
-
-def regroup_and_quantise(nc, pool, raw, codes, scales, name):
-    grouped = pool.tile([P, 4 * E], BF16, name=name, align_bytes=64)
-    nc.vector.tensor_copy(
-        out=grouped[:].rearrange("p (c i t) -> p c t i", i=4, t=4),
-        in_=raw[:].rearrange("p t (c i) -> p c t i", i=4),
-    )
-    nc.vector.quantize_mx(out=codes[:].bitcast(FP8X4), scales=scales[:], in_=grouped[:])
+LA = 3
+V_NORM = 4
 
 
 def tile_multiscaleretention_pb_t_kernel(tc, x, attn, Wg, bg, gn_w, gn_b, Wo, bo, out):
@@ -44,71 +33,14 @@ def tile_multiscaleretention_pb_t_kernel(tc, x, attn, Wg, bg, gn_w, gn_b, Wo, bo
     with ExitStack() as ctx:
         const = ctx.enter_context(tc.tile_pool(name="const", bufs=1))
         xin = ctx.enter_context(tc.tile_pool(name="xin", bufs=3))
-        ain = ctx.enter_context(tc.tile_pool(name="ain", bufs=LA + 5))
+        ain = ctx.enter_context(tc.tile_pool(name="ain", bufs=LA + 3))
         small = ctx.enter_context(tc.tile_pool(name="small", bufs=LA + 3))
-        work = ctx.enter_context(tc.tile_pool(name="work", bufs=2))
-        outp = ctx.enter_context(tc.tile_pool(name="outp", bufs=3))
-        single = ctx.enter_context(tc.tile_pool(name="single", bufs=1))
+        two = ctx.enter_context(tc.tile_pool(name="two", bufs=2))
+        three = ctx.enter_context(tc.tile_pool(name="three", bufs=3))
         psum = ctx.enter_context(tc.psum_pool(name="psum", bufs=4))
 
         x_t = {}
         a_t = {}
-
-        def load_x(m):
-            x_sb = xin.tile([P, J, E], BF16)
-            nc.sync.dma_start(out=x_sb[:], in_=xf[m * MT : (m + 1) * MT, :].rearrange("(p j) k -> p j k", j=J))
-            x_t[m] = x_sb
-
-        def load_a(m):
-            a_sb = ain.tile([P, J, E], BF16)
-            nc.sync.dma_start(out=a_sb[:], in_=af[m * MT : (m + 1) * MT, :].rearrange("(p j) k -> p j k", j=J))
-            a_t[m] = a_sb
-
-        wg_raw = const.tile([P, 4, E], BF16)
-        for u in range(2):
-            nc.sync.dma_start(
-                out=wg_raw[:, 2 * u : 2 * u + 2, :],
-                in_=Wg[256 * u : 256 * u + 256, :].rearrange("(q e) c -> q e c", e=2),
-            )
-        load_x(0)
-        load_a(0)
-        vrows = const.tile([P, P], BF16)
-        nc.vector.memset(vrows[:], 0.0)
-        nc.sync.dma_start(out=vrows[0:4, :], in_=bg.rearrange("(t p) -> t p", p=P))
-        nc.sync.dma_start(out=vrows[4:8, :], in_=gn_w.rearrange("(t p) -> t p", p=P))
-        nc.sync.dma_start(out=vrows[8:12, :], in_=gn_b.rearrange("(t p) -> t p", p=P))
-        wo_raw = const.tile([P, 4, E], BF16)
-        nc.sync.dma_start(out=wo_raw[:], in_=Wo.rearrange("(t p) n -> p t n", p=P))
-        load_a(1)
-        load_x(1)
-        for m in range(2, LA + 2):
-            load_a(m)
-        bo_bf = const.tile([P, E], BF16)
-        nc.sync.dma_start(out=bo_bf[:], in_=bo.partition_broadcast(P))
-
-        ident = const.tile([P, P], F32)
-        make_identity(nc, ident[:])
-        mhalf = const.tile([P, G * J], F32)
-        nc.vector.memset(mhalf[:], -0.5)
-        eps_col = const.tile([P, 1], F32)
-        nc.vector.memset(eps_col[:], EPS)
-
-        wg_c = const.tile([P, E], U32, align_bytes=64)
-        wg_s = const.tile([P, E], U8, align_bytes=64)
-        regroup_and_quantise(nc, const, wg_raw, wg_c, wg_s, "wg_grouped")
-        wo_c = const.tile([P, E], U32, align_bytes=64)
-        wo_s = const.tile([P, E], U8, align_bytes=64)
-        regroup_and_quantise(nc, const, wo_raw, wo_c, wo_s, "wo_grouped")
-
-        vrows32 = const.tile([P, P], F32)
-        nc.vector.tensor_copy(out=vrows32[:], in_=vrows[:])
-        vps = psum.tile([P, E], F32, tag="s")
-        nc.tensor.transpose(vps[:, 0:P], vrows32[:], ident[:])
-        cols = const.tile([P, 12], F32)
-        nc.vector.tensor_copy(out=cols[:], in_=vps[:, 0:12])
-        bo_b = const.tile([P, E], F32)
-        nc.vector.tensor_copy(out=bo_b[:], in_=bo_bf[:])
-
         xt_t = {}
         xg_t = {}
         st_t = {}
@@ -128,6 +60,60 @@ def tile_multiscaleretention_pb_t_kernel(tc, x, attn, Wg, bg, gn_w, gn_b, Wo, bo
         def ok(m):
             return 0 <= m < NM
 
+        def load_x(m):
+            x_sb = xin.tile([P, J, E], BF16)
+            nc.sync.dma_start(out=x_sb[:], in_=xf[m * MT : (m + 1) * MT, :].rearrange("(p j) k -> p j k", j=J))
+            x_t[m] = x_sb
+
+        def load_a(m):
+            a_sb = ain.tile([P, J, E], BF16)
+            nc.sync.dma_start(out=a_sb[:], in_=af[m * MT : (m + 1) * MT, :].rearrange("(p j) k -> p j k", j=J))
+            a_t[m] = a_sb
+
+        def regroup_and_quantise(raw, codes, scales, name):
+            grouped = const.tile([P, 4 * E], BF16, name=name, align_bytes=64)
+            nc.vector.tensor_copy(
+                out=grouped[:].rearrange("p (c i t) -> p c t i", i=4, t=4),
+                in_=raw[:].rearrange("p t (c i) -> p c t i", i=4),
+            )
+            nc.vector.quantize_mx(out=codes[:].bitcast(FP8X4), scales=scales[:], in_=grouped[:])
+
+        vrows = const.tile([P, P], BF16)
+        nc.vector.memset(vrows[:], 0.0)
+        nc.scalar.dma_start(out=vrows[0:4, :], in_=bg.rearrange("(t p) -> t p", p=P))
+        nc.scalar.dma_start(out=vrows[4:8, :], in_=gn_w.rearrange("(t p) -> t p", p=P))
+        nc.scalar.dma_start(out=vrows[8:12, :], in_=gn_b.rearrange("(t p) -> t p", p=P))
+        load_a(0)
+        load_x(0)
+        wg_raw = const.tile([P, 4, E], BF16)
+        for u in range(2):
+            nc.sync.dma_start(
+                out=wg_raw[:, 2 * u : 2 * u + 2, :],
+                in_=Wg[256 * u : 256 * u + 256, :].rearrange("(q e) c -> q e c", e=2),
+            )
+        wo_raw = const.tile([P, 4, E], BF16)
+        bo_bf = const.tile([P, E], BF16)
+
+        ident = const.tile([P, P], F32)
+        make_identity(nc, ident[:])
+        mhalf = const.tile([P, G * J], F32)
+        nc.vector.memset(mhalf[:], -0.5)
+
+        wg_c = const.tile([P, E], U32, align_bytes=64)
+        wg_s = const.tile([P, E], U8, align_bytes=64)
+        wo_c = const.tile([P, E], U32, align_bytes=64)
+        wo_s = const.tile([P, E], U8, align_bytes=64)
+        bo_b = const.tile([P, E], F32)
+        vrows32 = const.tile([P, P], F32)
+        cols = const.tile([P, 12], F32)
+
+        def prepare_wg_and_columns():
+            regroup_and_quantise(wg_raw, wg_c, wg_s, "wg_grouped")
+            nc.vector.tensor_copy(out=vrows32[:], in_=vrows[:])
+            vps = psum.tile([P, E], F32, tag="s")
+            nc.tensor.transpose(vps[:, 0:P], vrows32[:], ident[:])
+            nc.vector.tensor_copy(out=cols[:], in_=vps[:, 0:12])
+
         def x_transposes(m, hh):
             xt = psum.tile([P, 2, 256], F32, tag="s")
             for jj in range(2):
@@ -138,7 +124,7 @@ def tile_multiscaleretention_pb_t_kernel(tc, x, attn, Wg, bg, gn_w, gn_b, Wo, bo
 
         def x_copy_out(m, hh):
             if hh == 0:
-                xg = work.tile([P, 4 * MT], BF16, align_bytes=64)
+                xg = two.tile([P, 4 * MT], BF16, align_bytes=64)
                 xg_t[m] = xg
             xg_w = xg_t[m][:].bitcast(F32).rearrange("q (w u) -> q w u", u=2)
             nc.scalar.copy(out=xg_w[:, 256 * hh : 256 * hh + 256, :], in_=xt_t[(m, hh)][:].rearrange("q u w -> q w u"))
@@ -151,39 +137,38 @@ def tile_multiscaleretention_pb_t_kernel(tc, x, attn, Wg, bg, gn_w, gn_b, Wo, bo
                         out=st[:, j, gp, :],
                         in_=a_t[m][:, j, 256 * gp : 256 * gp + 256].rearrange("p (g c) -> p c g", g=2),
                     )
-            st_t[m] = st[:].rearrange("p j gp (s k) -> p (j gp s) k", k=3)
-
-        def rstd_ops(m):
-            st3 = st_t[m]
+            st3 = st[:].rearrange("p j gp (s k) -> p (j gp s) k", k=3)
             ve = small.tile([P, G * J], F32)
-            nc.scalar.activation(out=ve[:], in_=st3[:, :, 2], func=ACT.Identity, bias=eps_col[:], scale=1.0 / P)
+            nc.gpsimd.tensor_scalar(out=ve[:], in0=st3[:, :, 2], scalar1=1.0 / P, scalar2=EPS, op0=ALU.mult, op1=ALU.add)
             nm = small.tile([P, G * J], F32)
-            nc.scalar.mul(out=nm[:], in_=st3[:, :, 1], mul=-1.0)
+            nc.gpsimd.tensor_scalar(out=nm[:], in0=st3[:, :, 1], scalar1=-1.0, scalar2=0.0, op0=ALU.mult, op1=ALU.add)
             rstd = small.tile([P, G * J], F32)
             nc.gpsimd.tensor_tensor(out=rstd[:], in0=ve[:], in1=mhalf[:], op=ALU.pow)
             nb = small.tile([P, G * J], F32)
             nc.gpsimd.tensor_tensor(out=nb[:], in0=nm[:], in1=rstd[:], op=ALU.mult)
+            st_t[m] = st3
             rs_t[m] = rstd
             nb_t[m] = nb
 
-        def normalise(m, g):
-            if g == 0:
-                nrm = work.tile([P, J, E], F32)
-                nrm_t[m] = nrm
+        def normalise_v(m):
+            nrm = two.tile([P, J, E], F32)
+            nrm_t[m] = nrm
+            for j in range(V_NORM):
+                i = G * j
+                nc.vector.tensor_scalar(
+                    out=nrm[:, j, 0:P], in0=a_t[m][:, j, 0:P],
+                    scalar1=st_t[m][:, i, 1:2], scalar2=rs_t[m][:, i : i + 1],
+                    op0=ALU.subtract, op1=ALU.mult,
+                )
+
+        def normalise_s(m, g):
             cs = slice(P * g, P * g + P)
-            for j in range(J):
+            for j in range(V_NORM if g == 0 else 0, J):
                 i = G * j + g
-                if G * g + j < S_NORM:
-                    nc.scalar.activation(
-                        out=nrm_t[m][:, j, cs], in_=a_t[m][:, j, cs], func=ACT.Identity,
-                        bias=nb_t[m][:, i : i + 1], scale=rs_t[m][:, i : i + 1],
-                    )
-                else:
-                    nc.vector.tensor_scalar(
-                        out=nrm_t[m][:, j, cs], in0=a_t[m][:, j, cs],
-                        scalar1=st_t[m][:, i, 1:2], scalar2=rs_t[m][:, i : i + 1],
-                        op0=ALU.subtract, op1=ALU.mult,
-                    )
+                nc.scalar.activation(
+                    out=nrm_t[m][:, j, cs], in_=a_t[m][:, j, cs], func=ACT.Identity,
+                    bias=nb_t[m][:, i : i + 1], scale=rs_t[m][:, i : i + 1],
+                )
 
         def n_transposes(m, g):
             nt = psum.tile([P, MT], F32, tag="s")
@@ -193,7 +178,7 @@ def tile_multiscaleretention_pb_t_kernel(tc, x, attn, Wg, bg, gn_w, gn_b, Wo, bo
 
         def gain_bias(m, g):
             if g == 0:
-                gs = work.tile([P, G, MT], F32)
+                gs = three.tile([P, G, MT], F32)
                 gs_t[m] = gs
             nc.scalar.activation(
                 out=gs_t[m][:, g, :], in_=nt_t[(m, g)][:], func=ACT.Identity,
@@ -201,8 +186,8 @@ def tile_multiscaleretention_pb_t_kernel(tc, x, attn, Wg, bg, gn_w, gn_b, Wo, bo
             )
 
         def quantise_x(m):
-            xc = work.tile([P, MT], U32, align_bytes=64)
-            xs = work.tile([P, MT], U8, align_bytes=64)
+            xc = three.tile([P, MT], U32, align_bytes=64)
+            xs = three.tile([P, MT], U8, align_bytes=64)
             nc.vector.quantize_mx(out=xc[:].bitcast(FP8X4), scales=xs[:], in_=xg_t[m][:])
             xq_t[m] = (xc, xs)
 
@@ -218,35 +203,24 @@ def tile_multiscaleretention_pb_t_kernel(tc, x, attn, Wg, bg, gn_w, gn_b, Wo, bo
 
         def silu(m, t):
             if t == 0:
-                gate = work.tile([P, G, MT], F32)
+                gate = three.tile([P, G, MT], F32)
                 gate_t[m] = gate
             nc.scalar.activation(out=gate_t[m][:, t, :], in_=z_t[(m, t)][:], func=ACT.Silu, bias=cols[:, t : t + 1], scale=1.0)
 
-        def product_v(m):
-            hv = work.tile([P, 4 * TV], BF16, align_bytes=64)
+        def product(m):
+            h = two.tile([P, 4 * MT], BF16, align_bytes=64)
             nc.vector.tensor_tensor(
-                out=hv[:].rearrange("p (c i t) -> p c t i", i=4, t=4),
-                in0=gate_t[m][:, :, 0:TV].rearrange("p t (c i) -> p c t i", i=4),
-                in1=gs_t[m][:, :, 0:TV].rearrange("p t (c i) -> p c t i", i=4),
+                out=h[:].rearrange("p (c i t) -> p c t i", i=4, t=4),
+                in0=gate_t[m][:].rearrange("p t (c i) -> p c t i", i=4),
+                in1=gs_t[m][:].rearrange("p t (c i) -> p c t i", i=4),
                 op=ALU.mult,
             )
-            h_t[(m, 0)] = hv
-
-        def product_g(m):
-            hg = single.tile([P, 4 * (MT - TV)], BF16, align_bytes=64)
-            nc.gpsimd.tensor_tensor(
-                out=hg[:].rearrange("p (w t) -> p w t", t=4),
-                in0=gate_t[m][:, :, TV:MT].rearrange("p t w -> p w t"),
-                in1=gs_t[m][:, :, TV:MT].rearrange("p t w -> p w t"),
-                op=ALU.mult,
-            )
-            h_t[(m, 1)] = hg
+            h_t[m] = h
 
         def quantise_h(m):
-            hc = work.tile([P, MT], U32, align_bytes=64)
-            hs = work.tile([P, MT], U8, align_bytes=64)
-            nc.vector.quantize_mx(out=hc[:, 0:TV].bitcast(FP8X4), scales=hs[:, 0:TV], in_=h_t[(m, 0)][:])
-            nc.vector.quantize_mx(out=hc[:, TV:MT].bitcast(FP8X4), scales=hs[:, TV:MT], in_=h_t[(m, 1)][:])
+            hc = two.tile([P, MT], U32, align_bytes=64)
+            hs = two.tile([P, MT], U8, align_bytes=64)
+            nc.vector.quantize_mx(out=hc[:].bitcast(FP8X4), scales=hs[:], in_=h_t[m][:])
             hq_t[m] = (hc, hs)
 
         def matmul_2(m, j):
@@ -259,69 +233,69 @@ def tile_multiscaleretention_pb_t_kernel(tc, x, attn, Wg, bg, gn_w, gn_b, Wo, bo
             )
             o_t[(m, j)] = o
 
-        def add_bo(m, j):
+        def add_bo_and_store(m, j):
             if j == 0:
-                o_sb = outp.tile([P, J, E], F32)
+                o_sb = three.tile([P, J, E], F32)
                 ob_t[m] = o_sb
             nc.vector.tensor_tensor(out=ob_t[m][:, j, :], in0=o_t[(m, j)][:], in1=bo_b[:], op=ALU.add)
+            nc.sync.dma_start(
+                out=of[m * MT : (m + 1) * MT, :].rearrange("(p j) n -> p j n", j=J)[:, j, :], in_=ob_t[m][:, j, :]
+            )
 
-        def store(m):
-            nc.sync.dma_start(out=of[m * MT : (m + 1) * MT, :].rearrange("(p j) n -> p j n", j=J), in_=ob_t[m][:])
-
-        if PIN:
-            ctx.enter_context(tc.manual_schedule())
+        ctx.enter_context(tc.manual_schedule())
         for i in range(-LA, NM + 3):
             c = i - 1
-            d1 = i - 2
-            d2 = i - 3
-            if ok(i + 2) and i >= 0:
-                load_x(i + 2)
-            if ok(i + LA + 2) and i >= 0:
-                load_a(i + LA + 2)
-            if ok(i + LA - 1):
-                rstd_ops(i + LA - 1)
-            if ok(i):
-                x_copy_out(i, 0)
-                x_copy_out(i, 1)
-            if ok(d1):
-                product_v(d1)
+            d = i - 3
+            if ok(i + LA + 1):
+                load_a(i + LA + 1)
+            if ok(i + 4) and i + 4 >= 1:
+                load_x(i + 4)
+            if i == -LA + 1:
+                nc.sync.dma_start(out=wo_raw[:], in_=Wo.rearrange("(t p) n -> p t n", p=P))
+                nc.sync.dma_start(out=bo_bf[:], in_=bo.partition_broadcast(P))
+            if ok(i + 2):
+                x_copy_out(i + 2, 0)
+                x_copy_out(i + 2, 1)
             if ok(c):
-                quantise_x(c)
-                for g in range(G):
-                    normalise(c, g)
+                for t in range(G):
+                    matmul_1(c, t)
+                for t in range(G):
+                    silu(c, t)
+            if ok(d):
+                product(d)
+            if ok(i):
+                normalise_v(i)
+            if ok(d):
+                quantise_h(d)
+            if ok(i + 1):
+                quantise_x(i + 1)
+            if ok(c):
+                normalise_s(c, 0)
+                n_transposes(c, 0)
+            if ok(d):
+                for j in range(J):
+                    matmul_2(d, j)
+            if ok(c):
+                for g in range(1, G):
+                    normalise_s(c, g)
                     n_transposes(c, g)
                 gain_bias(c, 0)
-                matmul_1(c, 0)
+            if ok(i + 3):
+                x_transposes(i + 3, 0)
+            if ok(c):
                 gain_bias(c, 1)
-                matmul_1(c, 1)
+            if ok(i + 3):
+                x_transposes(i + 3, 1)
+            if ok(c):
                 gain_bias(c, 2)
-                matmul_1(c, 2)
-            if ok(d2):
-                quantise_h(d2)
-                matmul_2(d2, 0)
-                matmul_2(d2, 1)
-            if ok(d1):
-                product_g(d1)
-            if ok(c):
                 gain_bias(c, 3)
-                matmul_1(c, 3)
-            if ok(d2):
-                matmul_2(d2, 2)
-                matmul_2(d2, 3)
-            if ok(c):
-                silu(c, 0)
-            if ok(i + 1) and i >= -1:
-                x_transposes(i + 1, 0)
-            if ok(c):
-                silu(c, 1)
-            if ok(i + 1) and i >= -1:
-                x_transposes(i + 1, 1)
-            if ok(c):
-                silu(c, 2)
-                silu(c, 3)
             if ok(i + LA):
                 stats(i + LA)
-            if ok(d2):
+            if i == -LA:
+                prepare_wg_and_columns()
+            if i == 0:
+                regroup_and_quantise(wo_raw, wo_c, wo_s, "wo_grouped")
+                nc.vector.tensor_copy(out=bo_b[:], in_=bo_bf[:])
+            if ok(d):
                 for j in range(J):
-                    add_bo(d2, j)
-                store(d2)
+                    add_bo_and_store(d, j)

@@ -32,7 +32,7 @@ def tile_multiscaleretention_pb_t_kernel(tc, x, attn, Wg, bg, gn_w, gn_b, Wo, bo
     of = out.flatten_outer_dims()
     with ExitStack() as ctx:
         const = ctx.enter_context(tc.tile_pool(name="const", bufs=1))
-        xin = ctx.enter_context(tc.tile_pool(name="xin", bufs=3))
+        xin = ctx.enter_context(tc.tile_pool(name="xin", bufs=4))
         ain = ctx.enter_context(tc.tile_pool(name="ain", bufs=LA + 3))
         small = ctx.enter_context(tc.tile_pool(name="small", bufs=LA + 3))
         two = ctx.enter_context(tc.tile_pool(name="two", bufs=2))
@@ -91,8 +91,16 @@ def tile_multiscaleretention_pb_t_kernel(tc, x, attn, Wg, bg, gn_w, gn_b, Wo, bo
                 out=wg_raw[:, 2 * u : 2 * u + 2, :],
                 in_=Wg[256 * u : 256 * u + 256, :].rearrange("(q e) c -> q e c", e=2),
             )
+        load_x(1)
+        load_a(1)
+        load_x(2)
+        load_a(2)
+        load_x(3)
         wo_raw = const.tile([P, 4, E], BF16)
-        bo_bf = const.tile([P, E], BF16)
+        nc.sync.dma_start(out=wo_raw[:], in_=Wo.rearrange("(t p) n -> p t n", p=P))
+        load_a(3)
+        bo_b = const.tile([P, E], BF16)
+        nc.sync.dma_start(out=bo_b[:], in_=bo.partition_broadcast(P))
 
         ident = const.tile([P, P], F32)
         make_identity(nc, ident[:])
@@ -103,7 +111,6 @@ def tile_multiscaleretention_pb_t_kernel(tc, x, attn, Wg, bg, gn_w, gn_b, Wo, bo
         wg_s = const.tile([P, E], U8, align_bytes=64)
         wo_c = const.tile([P, E], U32, align_bytes=64)
         wo_s = const.tile([P, E], U8, align_bytes=64)
-        bo_b = const.tile([P, E], F32)
         vrows32 = const.tile([P, P], F32)
         cols = const.tile([P, 12], F32)
 
@@ -153,17 +160,20 @@ def tile_multiscaleretention_pb_t_kernel(tc, x, attn, Wg, bg, gn_w, gn_b, Wo, bo
         def normalise_v(m):
             nrm = two.tile([P, J, E], F32)
             nrm_t[m] = nrm
-            for j in range(V_NORM):
-                i = G * j
+            for gj in range(V_NORM):
+                g = gj // J
+                j = gj % J
+                i = G * j + g
+                cs = slice(P * g, P * g + P)
                 nc.vector.tensor_scalar(
-                    out=nrm[:, j, 0:P], in0=a_t[m][:, j, 0:P],
+                    out=nrm[:, j, cs], in0=a_t[m][:, j, cs],
                     scalar1=st_t[m][:, i, 1:2], scalar2=rs_t[m][:, i : i + 1],
                     op0=ALU.subtract, op1=ALU.mult,
                 )
 
         def normalise_s(m, g):
             cs = slice(P * g, P * g + P)
-            for j in range(V_NORM if g == 0 else 0, J):
+            for j in range(min(J, max(0, V_NORM - J * g)), J):
                 i = G * j + g
                 nc.scalar.activation(
                     out=nrm_t[m][:, j, cs], in_=a_t[m][:, j, cs], func=ACT.Identity,
@@ -246,21 +256,16 @@ def tile_multiscaleretention_pb_t_kernel(tc, x, attn, Wg, bg, gn_w, gn_b, Wo, bo
         for i in range(-LA, NM + 3):
             c = i - 1
             d = i - 3
-            if ok(i + LA + 1):
+            if ok(i + LA + 1) and i >= 0:
                 load_a(i + LA + 1)
-            if ok(i + 4) and i + 4 >= 1:
+            if ok(i + 4) and i >= 0:
                 load_x(i + 4)
-            if i == -LA + 1:
-                nc.sync.dma_start(out=wo_raw[:], in_=Wo.rearrange("(t p) n -> p t n", p=P))
-                nc.sync.dma_start(out=bo_bf[:], in_=bo.partition_broadcast(P))
             if ok(i + 2):
                 x_copy_out(i + 2, 0)
                 x_copy_out(i + 2, 1)
             if ok(c):
                 for t in range(G):
                     matmul_1(c, t)
-                for t in range(G):
-                    silu(c, t)
             if ok(d):
                 product(d)
             if ok(i):
@@ -269,14 +274,13 @@ def tile_multiscaleretention_pb_t_kernel(tc, x, attn, Wg, bg, gn_w, gn_b, Wo, bo
                 quantise_h(d)
             if ok(i + 1):
                 quantise_x(i + 1)
-            if ok(c):
-                normalise_s(c, 0)
-                n_transposes(c, 0)
             if ok(d):
                 for j in range(J):
                     matmul_2(d, j)
             if ok(c):
-                for g in range(1, G):
+                for t in range(G):
+                    silu(c, t)
+                for g in range(G):
                     normalise_s(c, g)
                     n_transposes(c, g)
                 gain_bias(c, 0)
@@ -295,7 +299,6 @@ def tile_multiscaleretention_pb_t_kernel(tc, x, attn, Wg, bg, gn_w, gn_b, Wo, bo
                 prepare_wg_and_columns()
             if i == 0:
                 regroup_and_quantise(wo_raw, wo_c, wo_s, "wo_grouped")
-                nc.vector.tensor_copy(out=bo_b[:], in_=bo_bf[:])
             if ok(d):
                 for j in range(J):
                     add_bo_and_store(d, j)

@@ -268,13 +268,10 @@ def tile_multiscaleretention_pb_t_kernel(tc, x, attn, Wg, bg, gn_w, gn_b, Wo, bo
                     matmul_1(c, t)
             if ok(d):
                 product(d)
-            if ok(i):
-                normalise_v(i)
-            if ok(d):
-                quantise_h(d)
             if ok(i + 1):
                 quantise_x(i + 1)
             if ok(d):
+                quantise_h(d)
                 for j in range(J):
                     matmul_2(d, j)
             if ok(c):
@@ -295,6 +292,8 @@ def tile_multiscaleretention_pb_t_kernel(tc, x, attn, Wg, bg, gn_w, gn_b, Wo, bo
                 gain_bias(c, 3)
             if ok(i + LA):
                 stats(i + LA)
+            if ok(i):
+                normalise_v(i)
             if i == -LA:
                 prepare_wg_and_columns()
             if i == 0:

@@ -44,6 +44,7 @@ def tile_multiscaleretention_pb_t_kernel(tc, x, attn, Wg, bg, gn_w, gn_b, Wo, bo
         xt_t = {}
         xg_t = {}
         st_t = {}
+        nm_t = {}
         rs_t = {}
         nb_t = {}
         xq_t = {}
@@ -145,15 +146,18 @@ def tile_multiscaleretention_pb_t_kernel(tc, x, attn, Wg, bg, gn_w, gn_b, Wo, bo
                         in_=a_t[m][:, j, 256 * gp : 256 * gp + 256].rearrange("p (g c) -> p c g", g=2),
                     )
             st3 = st[:].rearrange("p j gp (s k) -> p (j gp s) k", k=3)
-            ve = small.tile([P, G * J], F32)
-            nc.gpsimd.tensor_scalar(out=ve[:], in0=st3[:, :, 2], scalar1=1.0 / P, scalar2=EPS, op0=ALU.mult, op1=ALU.add)
             nm = small.tile([P, G * J], F32)
             nc.gpsimd.tensor_scalar(out=nm[:], in0=st3[:, :, 1], scalar1=-1.0, scalar2=0.0, op0=ALU.mult, op1=ALU.add)
+            st_t[m] = st3
+            nm_t[m] = nm
+
+        def finish_stats(m):
+            ve = small.tile([P, G * J], F32)
+            nc.vector.tensor_scalar(out=ve[:], in0=st_t[m][:, :, 2], scalar1=1.0 / P, scalar2=EPS, op0=ALU.mult, op1=ALU.add)
             rstd = small.tile([P, G * J], F32)
             nc.gpsimd.tensor_tensor(out=rstd[:], in0=ve[:], in1=mhalf[:], op=ALU.pow)
             nb = small.tile([P, G * J], F32)
-            nc.gpsimd.tensor_tensor(out=nb[:], in0=nm[:], in1=rstd[:], op=ALU.mult)
-            st_t[m] = st3
+            nc.gpsimd.tensor_tensor(out=nb[:], in0=nm_t[m][:], in1=rstd[:], op=ALU.mult)
             rs_t[m] = rstd
             nb_t[m] = nb
 
@@ -290,10 +294,12 @@ def tile_multiscaleretention_pb_t_kernel(tc, x, attn, Wg, bg, gn_w, gn_b, Wo, bo
             if ok(c):
                 gain_bias(c, 2)
                 gain_bias(c, 3)
-            if ok(i + LA):
-                stats(i + LA)
             if ok(i):
                 normalise_v(i)
+            if ok(i + LA - 1):
+                finish_stats(i + LA - 1)
+            if ok(i + LA):
+                stats(i + LA)
             if i == -LA:
                 prepare_wg_and_columns()
             if i == 0:

@@ -22,7 +22,7 @@ EPS = 1e-5
 FLOPS = 2 * 2 * T * E * E
 
 LA = 3
-V_NORM = 4
+V_NORM = 2
 
 
 def tile_multiscaleretention_pb_t_kernel(tc, x, attn, Wg, bg, gn_w, gn_b, Wo, bo, out):

@@ -232,8 +232,8 @@ def tile_multiscaleretention_pb_t_kernel(tc, x, attn, Wg, bg, gn_w, gn_b, Wo, bo
             h_t[m] = h
 
         def quantise_h(m):
-            hc = two.tile([P, MT], U32, align_bytes=64)
-            hs = two.tile([P, MT], U8, align_bytes=64)
+            hc = three.tile([P, MT], U32, align_bytes=64)
+            hs = three.tile([P, MT], U8, align_bytes=64)
             nc.vector.quantize_mx(out=hc[:].bitcast(FP8X4), scales=hs[:], in_=h_t[m][:])
             hq_t[m] = (hc, hs)
 
@@ -257,9 +257,10 @@ def tile_multiscaleretention_pb_t_kernel(tc, x, attn, Wg, bg, gn_w, gn_b, Wo, bo
             )
 
         ctx.enter_context(tc.manual_schedule())
-        for i in range(-LA, NM + 3):
+        for i in range(-LA, NM + 4):
             c = i - 1
             d = i - 3
+            e = i - 4
             if ok(i + LA + 1) and i >= 0:
                 load_a(i + LA + 1)
             if ok(i + 4) and i >= 0:
@@ -276,8 +277,9 @@ def tile_multiscaleretention_pb_t_kernel(tc, x, attn, Wg, bg, gn_w, gn_b, Wo, bo
                 quantise_x(i + 1)
             if ok(d):
                 quantise_h(d)
+            if ok(e):
                 for j in range(J):
-                    matmul_2(d, j)
+                    matmul_2(e, j)
             if ok(c):
                 for t in range(G):
                     silu(c, t)
@@ -304,6 +306,6 @@ def tile_multiscaleretention_pb_t_kernel(tc, x, attn, Wg, bg, gn_w, gn_b, Wo, bo
                 prepare_wg_and_columns()
             if i == 0:
                 regroup_and_quantise(wo_raw, wo_c, wo_s, "wo_grouped")
-            if ok(d):
+            if ok(e):
                 for j in range(J):
-                    add_bo_and_store(d, j)
+                    add_bo_and_store(e, j)

@@ -132,7 +132,7 @@ def tile_multiscaleretention_pb_t_kernel(tc, x, attn, Wg, bg, gn_w, gn_b, Wo, bo
 
         def x_copy_out(m, hh):
             if hh == 0:
-                xg = two.tile([P, 4 * MT], BF16, align_bytes=64)
+                xg = xin.tile([P, 4 * MT], BF16, align_bytes=64)
                 xg_t[m] = xg
             xg_w = xg_t[m][:].bitcast(F32).rearrange("q (w u) -> q w u", u=2)
             nc.scalar.copy(out=xg_w[:, 256 * hh : 256 * hh + 256, :], in_=xt_t[(m, hh)][:].rearrange("q u w -> q w u"))
@@ -273,7 +273,9 @@ def tile_multiscaleretention_pb_t_kernel(tc, x, attn, Wg, bg, gn_w, gn_b, Wo, bo
                     matmul_1(c, t)
             if ok(d):
                 product(d)
-            if ok(i + 1):
+            if i <= 0 and ok(i + 2):
+                quantise_x(i + 2)
+            if i >= 2 and ok(i + 1):
                 quantise_x(i + 1)
             if ok(d):
                 quantise_h(d)
@@ -298,11 +300,12 @@ def tile_multiscaleretention_pb_t_kernel(tc, x, attn, Wg, bg, gn_w, gn_b, Wo, bo
                 gain_bias(c, 3)
             if ok(i):
                 normalise_v(i)
-            if ok(i + LA - 1):
+            if ok(i + LA - 1) and i + LA - 1 > 0:
                 finish_stats(i + LA - 1)
             if ok(i + LA):
                 stats(i + LA)
             if i == -LA:
+                finish_stats(0)
                 prepare_wg_and_columns()
             if i == 0:
                 regroup_and_quantise(wo_raw, wo_c, wo_s, "wo_grouped")

@@ -22,6 +22,7 @@ EPS = 1e-5
 FLOPS = 2 * 2 * T * E * E
 
 LA = 3
+BY_SCALAR = NM - 2
 V_NORM = 2
 
 
@@ -84,6 +85,7 @@ def tile_multiscaleretention_pb_t_kernel(tc, x, attn, Wg, bg, gn_w, gn_b, Wo, bo
         nc.scalar.dma_start(out=vrows[0:4, :], in_=bg.rearrange("(t p) -> t p", p=P))
         nc.scalar.dma_start(out=vrows[4:8, :], in_=gn_w.rearrange("(t p) -> t p", p=P))
         nc.scalar.dma_start(out=vrows[8:12, :], in_=gn_b.rearrange("(t p) -> t p", p=P))
+        nc.scalar.dma_start(out=vrows[12:16, :], in_=bo.rearrange("(t p) -> t p", p=P))
         load_a(0)
         load_x(0)
         wg_raw = const.tile([P, 4, E], BF16)
@@ -113,14 +115,14 @@ def tile_multiscaleretention_pb_t_kernel(tc, x, attn, Wg, bg, gn_w, gn_b, Wo, bo
         wo_c = const.tile([P, E], U32, align_bytes=64)
         wo_s = const.tile([P, E], U8, align_bytes=64)
         vrows32 = const.tile([P, P], F32)
-        cols = const.tile([P, 12], F32)
+        cols = const.tile([P, 16], F32)
 
         def prepare_wg_and_columns():
             regroup_and_quantise(wg_raw, wg_c, wg_s, "wg_grouped")
             nc.vector.tensor_copy(out=vrows32[:], in_=vrows[:])
             vps = psum.tile([P, E], F32, tag="s")
             nc.tensor.transpose(vps[:, 0:P], vrows32[:], ident[:])
-            nc.vector.tensor_copy(out=cols[:], in_=vps[:, 0:12])
+            nc.vector.tensor_copy(out=cols[:], in_=vps[:, 0:16])
 
         def x_transposes(m, hh):
             xt = psum.tile([P, 2, 256], F32, tag="s")
@@ -256,6 +258,27 @@ def tile_multiscaleretention_pb_t_kernel(tc, x, attn, Wg, bg, gn_w, gn_b, Wo, bo
                 out=of[m * MT : (m + 1) * MT, :].rearrange("(p j) n -> p j n", j=J)[:, j, :], in_=ob_t[m][:, j, :]
             )
 
+        def out_by_scalar(m):
+            hc, hs = hq_t[m]
+            ot_sb = const.tile([P, G, MT], F32)
+            for b in range(G):
+                ot = psum.tile([P, MT], F32, tag="s")
+                nc.tensor.matmul_mx(
+                    out=ot[:],
+                    lhsT=wo_c[:, P * b : P * b + P].bitcast(FP8X4), lhsT_scale=wo_s[:, P * b : P * b + P],
+                    rhs=hc[:].bitcast(FP8X4), rhs_scale=hs[:], start=True, stop=True,
+                )
+                nc.scalar.activation(out=ot_sb[:, b, :], in_=ot[:], func=ACT.Identity, bias=cols[:, 12 + b : 13 + b], scale=1.0)
+            o_sb = three.tile([P, J, E], F32)
+            for j in range(J):
+                o = psum.tile([P, E], F32, tag="s")
+                for b in range(G):
+                    nc.tensor.transpose(o[:, P * b : P * b + P], ot_sb[:, b, P * j : P * j + P], ident[:])
+                nc.scalar.copy(out=o_sb[:, j, :], in_=o[:])
+                nc.sync.dma_start(
+                    out=of[m * MT : (m + 1) * MT, :].rearrange("(p j) n -> p j n", j=J)[:, j, :], in_=o_sb[:, j, :]
+                )
+
         ctx.enter_context(tc.manual_schedule())
         for i in range(-LA, NM + 4):
             c = i - 1
@@ -279,7 +302,7 @@ def tile_multiscaleretention_pb_t_kernel(tc, x, attn, Wg, bg, gn_w, gn_b, Wo, bo
                 quantise_x(i + 1)
             if ok(d):
                 quantise_h(d)
-            if ok(e):
+            if ok(e) and e != BY_SCALAR:
                 for j in range(J):
                     matmul_2(e, j)
             if ok(c):
@@ -309,6 +332,8 @@ def tile_multiscaleretention_pb_t_kernel(tc, x, attn, Wg, bg, gn_w, gn_b, Wo, bo
                 prepare_wg_and_columns()
             if i == 0:
                 regroup_and_quantise(wo_raw, wo_c, wo_s, "wo_grouped")
-            if ok(e):
+            if ok(e) and e != BY_SCALAR:
                 for j in range(J):
                     add_bo_and_store(e, j)
+            if d == BY_SCALAR:
+                out_by_scalar(d)

from contextlib import ExitStack

import concourse.mybir as mybir
from concourse.masks import make_identity

F32 = mybir.dt.float32
BF16 = mybir.dt.bfloat16
U32 = mybir.dt.uint32
U8 = mybir.dt.uint8
FP8X4 = mybir.dt.float8_e4m3fn_x4
ACT = mybir.ActivationFunctionType
ALU = mybir.AluOpType

P = 128
E = 512
T = 8192
G = 4
J = 4
MT = P * J
NM = T // MT
EPS = 1e-5
FLOPS = 2 * 2 * T * E * E

LA = 3
BY_SCALAR = NM - 2
V_NORM = 2


def tile_multiscaleretention_pb_t_kernel(tc, x, attn, Wg, bg, gn_w, gn_b, Wo, bo, out):
    nc = tc.nc
    xf = x.flatten_outer_dims()
    af = attn.flatten_outer_dims()
    of = out.flatten_outer_dims()
    with ExitStack() as ctx:
        const = ctx.enter_context(tc.tile_pool(name="const", bufs=1))
        xin = ctx.enter_context(tc.tile_pool(name="xin", bufs=4))
        ain = ctx.enter_context(tc.tile_pool(name="ain", bufs=LA + 3))
        small = ctx.enter_context(tc.tile_pool(name="small", bufs=LA + 3))
        two = ctx.enter_context(tc.tile_pool(name="two", bufs=2))
        three = ctx.enter_context(tc.tile_pool(name="three", bufs=3))
        psum = ctx.enter_context(tc.psum_pool(name="psum", bufs=4))

        x_t = {}
        a_t = {}
        xt_t = {}
        xg_t = {}
        st_t = {}
        nm_t = {}
        rs_t = {}
        nb_t = {}
        xq_t = {}
        nrm_t = {}
        nt_t = {}
        z_t = {}
        gate_t = {}
        gs_t = {}
        h_t = {}
        hq_t = {}
        o_t = {}
        ob_t = {}

        def ok(m):
            return 0 <= m < NM

        def load_x(m):
            x_sb = xin.tile([P, J, E], BF16)
            nc.sync.dma_start(out=x_sb[:], in_=xf[m * MT : (m + 1) * MT, :].rearrange("(p j) k -> p j k", j=J))
            x_t[m] = x_sb

        def load_a(m):
            a_sb = ain.tile([P, J, E], BF16)
            nc.sync.dma_start(out=a_sb[:], in_=af[m * MT : (m + 1) * MT, :].rearrange("(p j) k -> p j k", j=J))
            a_t[m] = a_sb

        def regroup_and_quantise(raw, codes, scales, name):
            grouped = const.tile([P, 4 * E], BF16, name=name, align_bytes=64)
            nc.vector.tensor_copy(
                out=grouped[:].rearrange("p (c i t) -> p c t i", i=4, t=4),
                in_=raw[:].rearrange("p t (c i) -> p c t i", i=4),
            )
            nc.vector.quantize_mx(out=codes[:].bitcast(FP8X4), scales=scales[:], in_=grouped[:])

        vrows = const.tile([P, P], BF16)
        nc.vector.memset(vrows[:], 0.0)
        nc.scalar.dma_start(out=vrows[0:4, :], in_=bg.rearrange("(t p) -> t p", p=P))
        nc.scalar.dma_start(out=vrows[4:8, :], in_=gn_w.rearrange("(t p) -> t p", p=P))
        nc.scalar.dma_start(out=vrows[8:12, :], in_=gn_b.rearrange("(t p) -> t p", p=P))
        nc.scalar.dma_start(out=vrows[12:16, :], in_=bo.rearrange("(t p) -> t p", p=P))
        load_a(0)
        load_x(0)
        wg_raw = const.tile([P, 4, E], BF16)
        for u in range(2):
            nc.sync.dma_start(
                out=wg_raw[:, 2 * u : 2 * u + 2, :],
                in_=Wg[256 * u : 256 * u + 256, :].rearrange("(q e) c -> q e c", e=2),
            )
        load_x(1)
        load_a(1)
        load_x(2)
        load_a(2)
        load_x(3)
        wo_raw = const.tile([P, 4, E], BF16)
        nc.sync.dma_start(out=wo_raw[:], in_=Wo.rearrange("(t p) n -> p t n", p=P))
        load_a(3)
        bo_b = const.tile([P, E], BF16)
        nc.sync.dma_start(out=bo_b[:], in_=bo.partition_broadcast(P))

        ident = const.tile([P, P], F32)
        make_identity(nc, ident[:])
        mhalf = const.tile([P, G * J], F32)
        nc.vector.memset(mhalf[:], -0.5)

        wg_c = const.tile([P, E], U32, align_bytes=64)
        wg_s = const.tile([P, E], U8, align_bytes=64)
        wo_c = const.tile([P, E], U32, align_bytes=64)
        wo_s = const.tile([P, E], U8, align_bytes=64)
        vrows32 = const.tile([P, P], F32)
        cols = const.tile([P, 16], F32)

        def prepare_wg_and_columns():
            regroup_and_quantise(wg_raw, wg_c, wg_s, "wg_grouped")
            nc.vector.tensor_copy(out=vrows32[:], in_=vrows[:])
            vps = psum.tile([P, E], F32, tag="s")
            nc.tensor.transpose(vps[:, 0:P], vrows32[:], ident[:])
            nc.vector.tensor_copy(out=cols[:], in_=vps[:, 0:16])

        def x_transposes(m, hh):
            xt = psum.tile([P, 2, 256], F32, tag="s")
            for jj in range(2):
                words = x_t[m][:, 2 * hh + jj, :].bitcast(F32)
                for u in range(2):
                    nc.tensor.transpose(xt[:, u, P * jj : P * jj + P], words[:, P * u : P * u + P], ident[:])
            xt_t[(m, hh)] = xt

        def x_copy_out(m, hh):
            if hh == 0:
                xg = xin.tile([P, 4 * MT], BF16, align_bytes=64)
                xg_t[m] = xg
            xg_w = xg_t[m][:].bitcast(F32).rearrange("q (w u) -> q w u", u=2)
            nc.scalar.copy(out=xg_w[:, 256 * hh : 256 * hh + 256, :], in_=xt_t[(m, hh)][:].rearrange("q u w -> q w u"))

        def stats(m):
            st = small.tile([P, J, 2, 6], F32)
            for j in range(J):
                for gp in range(2):
                    nc.vector.bn_stats(
                        out=st[:, j, gp, :],
                        in_=a_t[m][:, j, 256 * gp : 256 * gp + 256].rearrange("p (g c) -> p c g", g=2),
                    )
            st3 = st[:].rearrange("p j gp (s k) -> p (j gp s) k", k=3)
            nm = small.tile([P, G * J], F32)
            nc.gpsimd.tensor_scalar(out=nm[:], in0=st3[:, :, 1], scalar1=-1.0, scalar2=0.0, op0=ALU.mult, op1=ALU.add)
            st_t[m] = st3
            nm_t[m] = nm

        def finish_stats(m):
            ve = small.tile([P, G * J], F32)
            nc.vector.tensor_scalar(out=ve[:], in0=st_t[m][:, :, 2], scalar1=1.0 / P, scalar2=EPS, op0=ALU.mult, op1=ALU.add)
            rstd = small.tile([P, G * J], F32)
            nc.gpsimd.tensor_tensor(out=rstd[:], in0=ve[:], in1=mhalf[:], op=ALU.pow)
            nb = small.tile([P, G * J], F32)
            nc.gpsimd.tensor_tensor(out=nb[:], in0=nm_t[m][:], in1=rstd[:], op=ALU.mult)
            rs_t[m] = rstd
            nb_t[m] = nb

        def normalise_v(m):
            nrm = two.tile([P, J, E], F32)
            nrm_t[m] = nrm
            for gj in range(V_NORM):
                g = gj // J
                j = gj % J
                i = G * j + g
                cs = slice(P * g, P * g + P)
                nc.vector.tensor_scalar(
                    out=nrm[:, j, cs], in0=a_t[m][:, j, cs],
                    scalar1=st_t[m][:, i, 1:2], scalar2=rs_t[m][:, i : i + 1],
                    op0=ALU.subtract, op1=ALU.mult,
                )

        def normalise_s(m, g):
            cs = slice(P * g, P * g + P)
            for j in range(min(J, max(0, V_NORM - J * g)), J):
                i = G * j + g
                nc.scalar.activation(
                    out=nrm_t[m][:, j, cs], in_=a_t[m][:, j, cs], func=ACT.Identity,
                    bias=nb_t[m][:, i : i + 1], scale=rs_t[m][:, i : i + 1],
                )

        def n_transposes(m, g):
            nt = psum.tile([P, MT], F32, tag="s")
            for j in range(J):
                nc.tensor.transpose(nt[:, P * j : P * j + P], nrm_t[m][:, j, P * g : P * g + P], ident[:])
            nt_t[(m, g)] = nt

        def gain_bias(m, g):
            if g == 0:
                gs = three.tile([P, G, MT], F32)
                gs_t[m] = gs
            nc.scalar.activation(
                out=gs_t[m][:, g, :], in_=nt_t[(m, g)][:], func=ACT.Identity,
                bias=cols[:, 8 + g : 9 + g], scale=cols[:, 4 + g : 5 + g],
            )

        def quantise_x(m):
            xc = three.tile([P, MT], U32, align_bytes=64)
            xs = three.tile([P, MT], U8, align_bytes=64)
            nc.vector.quantize_mx(out=xc[:].bitcast(FP8X4), scales=xs[:], in_=xg_t[m][:])
            xq_t[m] = (xc, xs)

        def matmul_1(m, t):
            xc, xs = xq_t[m]
            z = psum.tile([P, MT], F32, tag="s")
            nc.tensor.matmul_mx(
                out=z[:],
                lhsT=wg_c[:, P * t : P * t + P].bitcast(FP8X4), lhsT_scale=wg_s[:, P * t : P * t + P],
                rhs=xc[:].bitcast(FP8X4), rhs_scale=xs[:], start=True, stop=True,
            )
            z_t[(m, t)] = z

        def silu(m, t):
            if t == 0:
                gate = three.tile([P, G, MT], F32)
                gate_t[m] = gate
            nc.scalar.activation(out=gate_t[m][:, t, :], in_=z_t[(m, t)][:], func=ACT.Silu, bias=cols[:, t : t + 1], scale=1.0)

        def product(m):
            h = two.tile([P, 4 * MT], BF16, align_bytes=64)
            nc.vector.tensor_tensor(
                out=h[:].rearrange("p (c i t) -> p c t i", i=4, t=4),
                in0=gate_t[m][:].rearrange("p t (c i) -> p c t i", i=4),
                in1=gs_t[m][:].rearrange("p t (c i) -> p c t i", i=4),
                op=ALU.mult,
            )
            h_t[m] = h

        def quantise_h(m):
            hc = three.tile([P, MT], U32, align_bytes=64)
            hs = three.tile([P, MT], U8, align_bytes=64)
            nc.vector.quantize_mx(out=hc[:].bitcast(FP8X4), scales=hs[:], in_=h_t[m][:])
            hq_t[m] = (hc, hs)

        def matmul_2(m, j):
            hc, hs = hq_t[m]
            o = psum.tile([P, E], F32, tag="o")
            nc.tensor.matmul_mx(
                out=o[:],
                lhsT=hc[:, P * j : P * j + P].bitcast(FP8X4), lhsT_scale=hs[:, P * j : P * j + P],
                rhs=wo_c[:].bitcast(FP8X4), rhs_scale=wo_s[:], start=True, stop=True,
            )
            o_t[(m, j)] = o

        def add_bo_and_store(m, j):
            if j == 0:
                o_sb = three.tile([P, J, E], F32)
                ob_t[m] = o_sb
            nc.vector.tensor_tensor(out=ob_t[m][:, j, :], in0=o_t[(m, j)][:], in1=bo_b[:], op=ALU.add)
            nc.sync.dma_start(
                out=of[m * MT : (m + 1) * MT, :].rearrange("(p j) n -> p j n", j=J)[:, j, :], in_=ob_t[m][:, j, :]
            )

        def out_by_scalar(m):
            hc, hs = hq_t[m]
            ot_sb = const.tile([P, G, MT], F32)
            for b in range(G):
                ot = psum.tile([P, MT], F32, tag="s")
                nc.tensor.matmul_mx(
                    out=ot[:],
                    lhsT=wo_c[:, P * b : P * b + P].bitcast(FP8X4), lhsT_scale=wo_s[:, P * b : P * b + P],
                    rhs=hc[:].bitcast(FP8X4), rhs_scale=hs[:], start=True, stop=True,
                )
                nc.scalar.activation(out=ot_sb[:, b, :], in_=ot[:], func=ACT.Identity, bias=cols[:, 12 + b : 13 + b], scale=1.0)
            o_sb = three.tile([P, J, E], F32)
            for j in range(J):
                o = psum.tile([P, E], F32, tag="s")
                for b in range(G):
                    nc.tensor.transpose(o[:, P * b : P * b + P], ot_sb[:, b, P * j : P * j + P], ident[:])
                nc.scalar.copy(out=o_sb[:, j, :], in_=o[:])
                nc.sync.dma_start(
                    out=of[m * MT : (m + 1) * MT, :].rearrange("(p j) n -> p j n", j=J)[:, j, :], in_=o_sb[:, j, :]
                )

        ctx.enter_context(tc.manual_schedule())
        for i in range(-LA, NM + 4):
            c = i - 1
            d = i - 3
            e = i - 4
            if ok(i + LA + 1) and i >= 0:
                load_a(i + LA + 1)
            if ok(i + 4) and i >= 0:
                load_x(i + 4)
            if ok(i + 2):
                x_copy_out(i + 2, 0)
                x_copy_out(i + 2, 1)
            if ok(c):
                for t in range(G):
                    matmul_1(c, t)
            if ok(d):
                product(d)
            if i <= 0 and ok(i + 2):
                quantise_x(i + 2)
            if i >= 2 and ok(i + 1):
                quantise_x(i + 1)
            if ok(d):
                quantise_h(d)
            if ok(e) and e != BY_SCALAR:
                for j in range(J):
                    matmul_2(e, j)
            if ok(c):
                for t in range(G):
                    silu(c, t)
                for g in range(G):
                    normalise_s(c, g)
                    n_transposes(c, g)
                gain_bias(c, 0)
            if ok(i + 3):
                x_transposes(i + 3, 0)
            if ok(c):
                gain_bias(c, 1)
            if ok(i + 3):
                x_transposes(i + 3, 1)
            if ok(c):
                gain_bias(c, 2)
                gain_bias(c, 3)
            if ok(i):
                normalise_v(i)
            if ok(i + LA - 1) and i + LA - 1 > 0:
                finish_stats(i + LA - 1)
            if ok(i + LA):
                stats(i + LA)
            if i == -LA:
                finish_stats(0)
                prepare_wg_and_columns()
            if i == 0:
                regroup_and_quantise(wo_raw, wo_c, wo_s, "wo_grouped")
            if ok(e) and e != BY_SCALAR:
                for j in range(J):
                    add_bo_and_store(e, j)
            if d == BY_SCALAR:
                out_by_scalar(d)
